import numpy as np
import ml_dtypes


def mxq(x, axis, fmt="e4m3"):
    dtype, down = {"e4m3": (ml_dtypes.float8_e4m3fn, 7), "e5m2": (ml_dtypes.float8_e5m2, 14)}[fmt]
    v = np.moveaxis(np.asarray(x, np.float32).astype(ml_dtypes.bfloat16).astype(np.float64), axis, -1)
    blocks = v.reshape(v.shape[:-1] + (-1, 32))
    amax = np.abs(blocks).max(-1, keepdims=True)
    byte = np.maximum(np.where(amax > 0, np.frexp(amax)[1] - 1 + 127, 0) - down, 1)
    scale = np.exp2(byte - 127.0)
    codes = (blocks / scale).astype(np.float32).astype(dtype).astype(np.float64)
    return np.moveaxis((codes * scale).reshape(v.shape), -1, axis)


BF16 = ml_dtypes.bfloat16


def bf(x):
    return np.asarray(x, np.float32).astype(BF16)


def f64(x):
    return np.asarray(x).astype(np.float64)


B, C, H, W, K, G = 2, 512, 64, 64, 512, 8
N = B * H * W
EPS = 1e-12


def l2norm(v):
    n = np.sqrt((v * v).sum(-1, keepdims=True))
    return v / np.maximum(n, EPS)


def setup_inputs():
    cen = np.random.standard_normal((G, C))
    sgn = np.sign(np.random.standard_normal((K, 1)))
    gain = np.exp(0.5 * np.random.standard_normal((K, 1)))
    memory = 0.5 * gain * (2.0 * sgn * cen[np.random.randint(0, G, K)] + np.random.standard_normal((K, C)))
    amp = 3.0 * np.random.random((N, 1))
    feat = amp * cen[np.random.randint(0, G, N)] + np.random.standard_normal((N, C))
    x = np.ascontiguousarray(feat.reshape(B, H, W, C).transpose(0, 3, 1, 2))
    return {"x": bf(x), "memory": bf(memory)}


def reference(x, memory):
    feat = f64(x).transpose(0, 2, 3, 1).reshape(N, C)
    feat_norm = l2norm(feat)
    mem_norm = l2norm(f64(memory))
    sim = mxq(feat_norm, 1, "e4m3") @ mxq(mem_norm, 1, "e4m3").T
    e = np.exp(sim - sim.max(1, keepdims=True))
    z = e.sum(1, keepdims=True)
    recon = (mxq(e, 1, "e4m3") @ mxq(mem_norm, 0, "e4m3")) / z
    match_map = (e / z).max(1)
    return recon.reshape(B, H, W, C).transpose(0, 3, 1, 2), match_map.reshape(B, H, W)

@@ -1,0 +1,394 @@
+from contextlib import ExitStack
+
+import concourse.mybir as mybir
+from concourse.masks import make_identity
+
+F32 = mybir.dt.float32
+BF16 = mybir.dt.bfloat16
+U32 = mybir.dt.uint32
+U8 = mybir.dt.uint8
+FP8X4 = mybir.dt.float8_e4m3fn_x4
+ALU = mybir.AluOpType
+ACT = mybir.ActivationFunctionType
+AX = mybir.AxisListType
+
+P = 128
+B, C, HW, K = 2, 512, 4096, 512
+CH = 512
+NCH = B * HW // CH
+LOADPX = 1024
+FLOPS = 2 * 2 * B * HW * C * K
+ETG = False
+A5G = False
+PIN = True
+
+
+def tile_memorybank2d_pa_t_kernel(tc, x, memory, out_0, out_1):
+    nc = tc.nc
+    with ExitStack() as ctx:
+        const = ctx.enter_context(tc.tile_pool(name="const", bufs=1))
+        xpool = ctx.enter_context(tc.tile_pool(name="xpool", bufs=1))
+        small = ctx.enter_context(tc.tile_pool(name="small", bufs=4))
+        work = ctx.enter_context(tc.tile_pool(name="work", bufs=2))
+        opool = ctx.enter_context(tc.tile_pool(name="opool", bufs=3))
+        psum = ctx.enter_context(tc.psum_pool(name="psum", bufs=1))
+        if PIN:
+            ctx.enter_context(tc.manual_schedule())
+
+        mem = const.tile([P, 4, C], BF16, name="mem")
+        nc.sync.dma_start(out=mem[:], in_=memory.rearrange("(p t) c -> p t c", t=4))
+        xs = []
+        for ld in range(B * HW // LOADPX):
+            b = ld // (HW // LOADPX)
+            n0 = (ld % (HW // LOADPX)) * LOADPX
+            x_sb = xpool.tile([P, 4, LOADPX], BF16, name="x%d" % ld)
+            nc.sync.dma_start(
+                out=x_sb[:],
+                in_=x[b].rearrange("(p j) h w -> p j (h w)", j=4)[:, :, n0 : n0 + LOADPX],
+            )
+            xs.append(x_sb)
+
+        ident_f = const.tile([P, P], F32, name="ident_f")
+        make_identity(nc, ident_f[:])
+        ident_b = const.tile([P, P], BF16, name="ident_b")
+        make_identity(nc, ident_b[:])
+        neghalf = const.tile([P, 4], F32, name="neghalf")
+        nc.vector.memset(neghalf[:], -0.5)
+        junk = const.tile([P, 512], BF16, name="junk")
+
+        mn = const.tile([P, 4, C], BF16, name="mn")
+        mnj = const.tile([P, 4, 4, P], BF16, name="mnj")
+        g2 = const.tile([P, C, 4], BF16, name="g2", align_bytes=64)
+        gm = const.tile([P, K, 4], BF16, name="gm", align_bytes=64)
+        mn2c = const.tile([P, C], U32, name="mn2c", align_bytes=64)
+        mn2s = const.tile([P, C], U8, name="mn2s", align_bytes=64)
+        mnTc = const.tile([P, K], U32, name="mnTc", align_bytes=64)
+        mnTs = const.tile([P, K], U8, name="mnTs", align_bytes=64)
+        ssm = const.tile([P, 4], F32, name="ssm")
+        ssmc = const.tile([P, 4], F32, name="ssmc")
+        rm = const.tile([P, 4], F32, name="rm")
+
+        st = {}
+
+        def ok(i):
+            return 0 <= i < NCH
+
+        def where(i):
+            return i // (HW // CH), (i % (HW // CH)) * CH
+
+        def xchunk(i):
+            per = LOADPX // CH
+            return xs[i // per], (i % per) * CH
+
+        def rsqrt_clamped(out, tmp, ss):
+            nc.gpsimd.tensor_scalar(out=tmp, in0=ss, scalar1=1e-24, scalar2=None, op0=ALU.max)
+            nc.gpsimd.tensor_tensor(out=out, in0=tmp, in1=neghalf[:], op=ALU.pow)
+
+        def TX(i, g):
+            if not ok(i):
+                return
+            x_sb, c0 = xchunk(i)
+            if g == 0:
+                st[("ss", i)] = small.tile([P, 4], F32, name="ss", tag="ss")
+            xt = psum.tile([P, 4, P], F32, name="xt", tag="xt", bufs=1)
+            w0 = c0 // 2 + P * g
+            for j in range(4):
+                nc.tensor.transpose(out=xt[:, j, :], in_=x_sb[:].bitcast(F32)[:, j, w0 : w0 + P], identity=ident_f[:])
+            st[("xt", i, g)] = xt
+
+        def SQ(i, g, e):
+            if not ok(i):
+                return
+            xt = st[("xt", i, g)]
+            ss = st[("ss", i)]
+            xv = xt[:].bitcast(BF16).rearrange("p j (q e) -> p j q e", e=2)
+            nc.scalar.activation(
+                out=junk[:].rearrange("p (j q) -> p j q", j=4),
+                in_=xv[:, :, :, e],
+                func=ACT.Square,
+                accum_out=ss[:, 2 * g + e : 2 * g + e + 1],
+            )
+
+        def R(i):
+            if not ok(i):
+                return
+            ssc = small.tile([P, 4], F32, name="ssc", tag="ssc")
+            r = small.tile([P, 4], F32, name="r", tag="r")
+            rsqrt_clamped(r[:], ssc[:], st[("ss", i)][:])
+            st[("r", i)] = r
+
+        def TB(i):
+            if not ok(i):
+                return
+            r = st[("r", i)]
+            rb = psum.tile([P, 4, P], F32, name="rb", tag="bc", bufs=2)
+            for col in range(4):
+                nc.tensor.transpose(out=rb[:, col, :], in_=r[:, col : col + 1].to_broadcast([P, P]), identity=ident_f[:])
+            st[("rb", i)] = rb
+            st[("gx", i)] = work.tile([P, CH, 4], BF16, name="gx", tag="gx", align_bytes=64)
+
+        def XR(i):
+            if not (ok(i) and A5G):
+                return
+            rbs = work.tile([P, P, 2], F32, name="rbs", tag="rbs")
+            nc.scalar.copy(out=rbs[:], in_=st[("rb", i)][:, 2:4, :].rearrange("p e q -> p q e"))
+            st[("rbs", i)] = rbs
+
+        def A5(i, g):
+            if not ok(i):
+                return
+            x_sb, c0 = xchunk(i)
+            gx = st[("gx", i)]
+            lo = 256 * g
+            if A5G and g == 1:
+                nc.gpsimd.tensor_tensor(
+                    out=gx[:, lo : lo + 256, :],
+                    in0=st[("rbs", i)][:].rearrange("p q e -> p (q e)").unsqueeze(2).to_broadcast([P, 256, 4]),
+                    in1=x_sb[:, :, c0 + lo : c0 + lo + 256].rearrange("p j n -> p n j"),
+                    op=ALU.mult,
+                )
+                return
+            nc.vector.tensor_tensor(
+                out=gx[:, lo : lo + 256, :].rearrange("p (q e) j -> p q e j", e=2),
+                in0=st[("rb", i)][:, 2 * g : 2 * g + 2, :].rearrange("p e q -> p q e").unsqueeze(3).to_broadcast([P, P, 2, 4]),
+                in1=x_sb[:, :, c0 + lo : c0 + lo + 256].rearrange("p j (q e) -> p q e j", e=2),
+                op=ALU.mult,
+            )
+
+        def QF(i):
+            if not ok(i):
+                return
+            fnc = work.tile([P, CH], U32, name="fnc", tag="fnc", align_bytes=64)
+            fns = work.tile([P, CH], U8, name="fns", tag="fns", align_bytes=64)
+            nc.vector.quantize_mx(out=fnc[:].bitcast(FP8X4), scales=fns[:], in_=st[("gx", i)][:].rearrange("p n j -> p (n j)"))
+            st[("fn", i)] = (fnc, fns)
+
+        def M1(i, k):
+            if not ok(i):
+                return
+            fnc, fns = st[("fn", i)]
+            if k == 0:
+                st[("negm", i)] = small.tile([P, 4], F32, name="negm", tag="negm")
+                st[("z", i)] = small.tile([P, 4], F32, name="z", tag="z")
+                st[("e", i)] = work.tile([P, 4, K], BF16, name="e", tag="e")
+            sim = psum.tile([P, K], F32, name="sim", tag="sim", bufs=2)
+            nc.tensor.matmul_mx(
+                out=sim[:],
+                lhsT=fnc[:, P * k : P * k + P].bitcast(FP8X4),
+                lhsT_scale=fns[:, P * k : P * k + P],
+                rhs=mnTc[:].bitcast(FP8X4),
+                rhs_scale=mnTs[:],
+                start=True,
+                stop=True,
+            )
+            st[("sim", i, k)] = sim
+
+        def MAX(i, k):
+            if not ok(i):
+                return
+            nc.vector.tensor_reduce(
+                out=st[("negm", i)][:, k : k + 1], in_=st[("sim", i, k)][:], axis=AX.X, op=ALU.max, negate=True
+            )
+
+        def EXP(i, k):
+            if not ok(i):
+                return
+            nc.scalar.activation(
+                out=st[("e", i)][:, k, :],
+                in_=st[("sim", i, k)][:],
+                func=ACT.Exp,
+                bias=st[("negm", i)][:, k : k + 1],
+                scale=1.0,
+                accum_out=st[("z", i)][:, k : k + 1],
+            )
+
+        def TE(i, h):
+            if not ok(i):
+                return
+            e = st[("e", i)]
+            if h == 0:
+                st[("ge", i)] = work.tile([P, CH, 4], BF16, name="ge", tag="ge", align_bytes=64)
+            et = psum.tile([P, 4, 256], BF16, name="et", tag="et", bufs=1)
+            for bb in range(2):
+                for t in range(4):
+                    nc.tensor.transpose(
+                        out=et[:, t, P * bb : P * bb + P], in_=e[:, 2 * h + bb, P * t : P * t + P], identity=ident_b[:]
+                    )
+            st[("et", i, h)] = et
+
+        def XE(i, h):
+            if not ok(i):
+                return
+            et = st[("et", i, h)]
+            dst = st[("ge", i)][:, 256 * h : 256 * h + 256, :]
+            if ETG:
+                ets = work.tile([P, 4, 256], BF16, name="ets", tag="ets")
+                nc.scalar.copy(out=ets[:], in_=et[:])
+                nc.gpsimd.tensor_scalar(
+                    out=dst, in0=ets[:].rearrange("p t n -> p n t"), scalar1=1.0, scalar2=0.0, op0=ALU.mult, op1=ALU.add
+                )
+            else:
+                nc.scalar.copy(out=dst, in_=et[:].rearrange("p t n -> p n t"))
+
+        def RZ(i):
+            if not ok(i):
+                return
+            rz = small.tile([P, 4], F32, name="rz", tag="rz")
+            nc.vector.reciprocal(out=rz[:], in_=st[("z", i)][:])
+            st[("rz", i)] = rz
+
+        def TZ(i):
+            if not ok(i):
+                return
+            rz = st[("rz", i)]
+            rzp = psum.tile([P, 4, P], F32, name="rzp", tag="bc", bufs=2)
+            for k in range(4):
+                nc.tensor.transpose(out=rzp[:, k, :], in_=rz[:, k : k + 1].to_broadcast([P, P]), identity=ident_f[:])
+            st[("rzp", i)] = rzp
+
+        def XZ(i):
+            if not ok(i):
+                return
+            b, n0 = where(i)
+            rzb = work.tile([P, CH], F32, name="rzb", tag="rzb", bufs=3)
+            nc.scalar.copy(out=rzb[:], in_=st[("rzp", i)][:].rearrange("p k n -> p (k n)"))
+            nc.sync.dma_start(out=out_1.rearrange("b h w -> b (h w)")[b : b + 1, n0 : n0 + CH], in_=rzb[0:1, :])
+            st[("rzb", i)] = rzb
+
+        def QE(i):
+            if not ok(i):
+                return
+            ec = work.tile([P, CH], U32, name="ec", tag="ec", align_bytes=64)
+            es = work.tile([P, CH], U8, name="es", tag="es", align_bytes=64)
+            nc.vector.quantize_mx(out=ec[:].bitcast(FP8X4), scales=es[:], in_=st[("ge", i)][:].rearrange("p n t -> p (n t)"))
+            st[("ec", i)] = (ec, es)
+
+        def M2(i, cc):
+            if not ok(i):
+                return
+            ec, es = st[("ec", i)]
+            if ("osb", i) not in st:
+                st[("osb", i)] = opool.tile([P, 4, CH], F32, name="osb", tag="osb")
+            rec = psum.tile([P, CH], F32, name="rec", tag="rec", bufs=2)
+            nc.tensor.matmul_mx(
+                out=rec[:],
+                lhsT=mn2c[:, P * cc : P * cc + P].bitcast(FP8X4),
+                lhsT_scale=mn2s[:, P * cc : P * cc + P],
+                rhs=ec[:].bitcast(FP8X4),
+                rhs_scale=es[:],
+                start=True,
+                stop=True,
+            )
+            st[("rec", i, cc)] = rec
+
+        def D(i, cc):
+            if not ok(i):
+                return
+            nc.vector.tensor_tensor(
+                out=st[("osb", i)][:, cc, :], in0=st[("rec", i, cc)][:], in1=st[("rzb", i)][:], op=ALU.mult
+            )
+
+        def STORE(i):
+            if not ok(i):
+                return
+            b, n0 = where(i)
+            nc.sync.dma_start(
+                out=out_0[b].rearrange("(cc p) h w -> p cc (h w)", p=P)[:, :, n0 : n0 + CH], in_=st[("osb", i)][:]
+            )
+
+        def MN2(part):
+            if part == 0:
+                for t in range(4):
+                    nc.vector.tensor_scalar(
+                        out=mn[:, t, :], in0=mem[:, t, :], scalar1=rm[:, t : t + 1], scalar2=None, op0=ALU.mult
+                    )
+            elif part == 1:
+                nc.vector.tensor_copy(out=g2[:], in_=mn[:].rearrange("p t c -> p c t"))
+            elif part == 2:
+                nc.vector.quantize_mx(out=mn2c[:].bitcast(FP8X4), scales=mn2s[:], in_=g2[:].rearrange("p c t -> p (c t)"))
+
+        def stage_a(i):
+            for g in range(2):
+                TX(i, g)
+                SQ(i, g, 0)
+                SQ(i, g, 1)
+            R(i)
+
+        for t in range(4):
+            nc.scalar.activation(out=junk[:], in_=mem[:, t, :], func=ACT.Square, accum_out=ssm[:, t : t + 1])
+        rsqrt_clamped(rm[:], ssmc[:], ssm[:])
+        stage_a(0)
+        stage_a(1)
+        for t in range(4):
+            nc.vector.tensor_scalar(
+                out=mnj[:, t, :, :],
+                in0=mem[:, t, :].rearrange("p (q j) -> p j q", j=4),
+                scalar1=rm[:, t : t + 1],
+                scalar2=None,
+                op0=ALU.mult,
+            )
+        TB(0)
+        XR(0)
+        tms = []
+        for h in range(2):
+            tm = psum.tile([P, 4, 256], BF16, name="tm", tag="sim", bufs=2)
+            for j in range(4):
+                for tt in range(2):
+                    nc.tensor.transpose(
+                        out=tm[:, j, P * tt : P * tt + P], in_=mnj[:, 2 * h + tt, j, :], identity=ident_b[:]
+                    )
+            tms.append(tm)
+        A5(0, 1)
+        A5(0, 0)
+        for h in range(2):
+            nc.scalar.copy(out=gm[:, 256 * h : 256 * h + 256, :], in_=tms[h][:].rearrange("p j s -> p s j"))
+        QF(0)
+        nc.vector.quantize_mx(out=mnTc[:].bitcast(FP8X4), scales=mnTs[:], in_=gm[:].rearrange("p s j -> p (s j)"))
+
+        for s in range(2, NCH + 3):
+            M1(s - 2, 0)
+            MAX(s - 2, 0)
+            M1(s - 2, 1)
+            MAX(s - 2, 1)
+            TX(s, 0)
+            EXP(s - 2, 0)
+            TB(s - 1)
+            QE(s - 3)
+            EXP(s - 2, 1)
+            M1(s - 2, 2)
+            SQ(s, 0, 0)
+            M2(s - 3, 1)
+            TE(s - 2, 0)
+            M1(s - 2, 3)
+            A5(s - 1, 0)
+            SQ(s, 0, 1)
+            MAX(s - 2, 2)
+            M2(s - 3, 0)
+            XE(s - 2, 0)
+            EXP(s - 2, 2)
+            D(s - 3, 1)
+            if s == 2:
+                MN2(0)
+            MAX(s - 2, 3)
+            TX(s, 1)
+            D(s - 3, 0)
+            if s == 2:
+                MN2(1)
+            A5(s - 1, 1)
+            EXP(s - 2, 3)
+            M2(s - 3, 2)
+            TE(s - 2, 1)
+            RZ(s - 2)
+            SQ(s, 1, 1)
+            M2(s - 3, 3)
+            QF(s - 1)
+            D(s - 3, 2)
+            if s == 2:
+                MN2(2)
+            SQ(s, 1, 0)
+            XE(s - 2, 1)
+            D(s - 3, 3)
+            STORE(s - 3)
+            R(s)
+            TZ(s - 2)
+            XZ(s - 2)

@@ -19,8 +19,9 @@ NCH = B * HW // CH
 LOADPX = 1024
 FLOPS = 2 * 2 * B * HW * C * K
 ETG = False
-A5G = False
+GP = (1, 2, 3)
 PIN = True
+NB = {"ss": 3, "r": 3, "gx": 3, "fn": 3, "e": 2, "ge": 4, "rz": 2, "rzb": 4, "ec": 2, "osb": 2, "rbs": 3}
 
 
 def tile_memorybank2d_pa_t_kernel(tc, x, memory, out_0, out_1):
@@ -89,7 +90,7 @@ def tile_memorybank2d_pa_t_kernel(tc, x, memory, out_0, out_1):
                 return
             x_sb, c0 = xchunk(i)
             if g == 0:
-                st[("ss", i)] = small.tile([P, 4], F32, name="ss", tag="ss")
+                st[("ss", i)] = small.tile([P, 4], F32, name="ss", tag="ss", bufs=NB["ss"])
             xt = psum.tile([P, 4, P], F32, name="xt", tag="xt", bufs=1)
             w0 = c0 // 2 + P * g
             for j in range(4):
@@ -112,8 +113,8 @@ def tile_memorybank2d_pa_t_kernel(tc, x, memory, out_0, out_1):
         def R(i):
             if not ok(i):
                 return
-            ssc = small.tile([P, 4], F32, name="ssc", tag="ssc")
-            r = small.tile([P, 4], F32, name="r", tag="r")
+            ssc = small.tile([P, 4], F32, name="ssc", tag="ssc", bufs=NB["r"])
+            r = small.tile([P, 4], F32, name="r", tag="r", bufs=NB["r"])
             rsqrt_clamped(r[:], ssc[:], st[("ss", i)][:])
             st[("r", i)] = r
 
@@ -125,41 +126,48 @@ def tile_memorybank2d_pa_t_kernel(tc, x, memory, out_0, out_1):
             for col in range(4):
                 nc.tensor.transpose(out=rb[:, col, :], in_=r[:, col : col + 1].to_broadcast([P, P]), identity=ident_f[:])
             st[("rb", i)] = rb
-            st[("gx", i)] = work.tile([P, CH, 4], BF16, name="gx", tag="gx", align_bytes=64)
+            st[("gx", i)] = work.tile([P, CH, 4], BF16, name="gx", tag="gx", align_bytes=64, bufs=NB["gx"])
 
         def XR(i):
-            if not (ok(i) and A5G):
+            if not (ok(i) and len(GP) > 0):
                 return
-            rbs = work.tile([P, P, 2], F32, name="rbs", tag="rbs")
-            nc.scalar.copy(out=rbs[:], in_=st[("rb", i)][:, 2:4, :].rearrange("p e q -> p q e"))
+            rbs = work.tile([P, CH], F32, name="rbs", tag="rbs", bufs=NB["rbs"])
+            nc.vector.tensor_copy(
+                out=rbs[:].rearrange("p (g q e) -> p g q e", g=2, e=2),
+                in_=st[("rb", i)][:].rearrange("p (g e) q -> p g q e", e=2),
+            )
             st[("rbs", i)] = rbs
 
-        def A5(i, g):
+        def A5(i, k):
             if not ok(i):
                 return
             x_sb, c0 = xchunk(i)
             gx = st[("gx", i)]
-            lo = 256 * g
-            if A5G and g == 1:
+            lo = P * k
+            if k in GP:
                 nc.gpsimd.tensor_tensor(
-                    out=gx[:, lo : lo + 256, :],
-                    in0=st[("rbs", i)][:].rearrange("p q e -> p (q e)").unsqueeze(2).to_broadcast([P, 256, 4]),
-                    in1=x_sb[:, :, c0 + lo : c0 + lo + 256].rearrange("p j n -> p n j"),
+                    out=gx[:, lo : lo + P, :],
+                    in0=st[("rbs", i)][:, lo : lo + P].unsqueeze(2).to_broadcast([P, P, 4]),
+                    in1=x_sb[:, :, c0 + lo : c0 + lo + P].rearrange("p j n -> p n j"),
                     op=ALU.mult,
                 )
                 return
+            g, q0 = k // 2, 64 * (k % 2)
             nc.vector.tensor_tensor(
-                out=gx[:, lo : lo + 256, :].rearrange("p (q e) j -> p q e j", e=2),
-                in0=st[("rb", i)][:, 2 * g : 2 * g + 2, :].rearrange("p e q -> p q e").unsqueeze(3).to_broadcast([P, P, 2, 4]),
-                in1=x_sb[:, :, c0 + lo : c0 + lo + 256].rearrange("p j (q e) -> p q e j", e=2),
+                out=gx[:, lo : lo + P, :].rearrange("p (q e) j -> p q e j", e=2),
+                in0=st[("rb", i)][:, 2 * g : 2 * g + 2, q0 : q0 + 64]
+                .rearrange("p e q -> p q e")
+                .unsqueeze(3)
+                .to_broadcast([P, 64, 2, 4]),
+                in1=x_sb[:, :, c0 + lo : c0 + lo + P].rearrange("p j (q e) -> p q e j", e=2),
                 op=ALU.mult,
             )
 
         def QF(i):
             if not ok(i):
                 return
-            fnc = work.tile([P, CH], U32, name="fnc", tag="fnc", align_bytes=64)
-            fns = work.tile([P, CH], U8, name="fns", tag="fns", align_bytes=64)
+            fnc = work.tile([P, CH], U32, name="fnc", tag="fnc", align_bytes=64, bufs=NB["fn"])
+            fns = work.tile([P, CH], U8, name="fns", tag="fns", align_bytes=64, bufs=NB["fn"])
             nc.vector.quantize_mx(out=fnc[:].bitcast(FP8X4), scales=fns[:], in_=st[("gx", i)][:].rearrange("p n j -> p (n j)"))
             st[("fn", i)] = (fnc, fns)
 
@@ -167,10 +175,10 @@ def tile_memorybank2d_pa_t_kernel(tc, x, memory, out_0, out_1):
             if not ok(i):
                 return
             fnc, fns = st[("fn", i)]
-            if k == 0:
-                st[("negm", i)] = small.tile([P, 4], F32, name="negm", tag="negm")
-                st[("z", i)] = small.tile([P, 4], F32, name="z", tag="z")
-                st[("e", i)] = work.tile([P, 4, K], BF16, name="e", tag="e")
+            if ("e", i) not in st:
+                st[("negm", i)] = small.tile([P, 4], F32, name="negm", tag="negm", bufs=NB["e"])
+                st[("z", i)] = small.tile([P, 4], F32, name="z", tag="z", bufs=NB["e"])
+                st[("e", i)] = work.tile([P, 4, K], BF16, name="e", tag="e", bufs=NB["e"])
             sim = psum.tile([P, K], F32, name="sim", tag="sim", bufs=2)
             nc.tensor.matmul_mx(
                 out=sim[:],
@@ -207,7 +215,7 @@ def tile_memorybank2d_pa_t_kernel(tc, x, memory, out_0, out_1):
                 return
             e = st[("e", i)]
             if h == 0:
-                st[("ge", i)] = work.tile([P, CH, 4], BF16, name="ge", tag="ge", align_bytes=64)
+                st[("ge", i)] = work.tile([P, CH, 4], BF16, name="ge", tag="ge", align_bytes=64, bufs=NB["ge"])
             et = psum.tile([P, 4, 256], BF16, name="et", tag="et", bufs=1)
             for bb in range(2):
                 for t in range(4):
@@ -233,7 +241,7 @@ def tile_memorybank2d_pa_t_kernel(tc, x, memory, out_0, out_1):
         def RZ(i):
             if not ok(i):
                 return
-            rz = small.tile([P, 4], F32, name="rz", tag="rz")
+            rz = small.tile([P, 4], F32, name="rz", tag="rz", bufs=NB["rz"])
             nc.vector.reciprocal(out=rz[:], in_=st[("z", i)][:])
             st[("rz", i)] = rz
 
@@ -250,7 +258,7 @@ def tile_memorybank2d_pa_t_kernel(tc, x, memory, out_0, out_1):
             if not ok(i):
                 return
             b, n0 = where(i)
-            rzb = work.tile([P, CH], F32, name="rzb", tag="rzb", bufs=3)
+            rzb = work.tile([P, CH], F32, name="rzb", tag="rzb", bufs=NB["rzb"])
             nc.scalar.copy(out=rzb[:], in_=st[("rzp", i)][:].rearrange("p k n -> p (k n)"))
             nc.sync.dma_start(out=out_1.rearrange("b h w -> b (h w)")[b : b + 1, n0 : n0 + CH], in_=rzb[0:1, :])
             st[("rzb", i)] = rzb
@@ -258,8 +266,8 @@ def tile_memorybank2d_pa_t_kernel(tc, x, memory, out_0, out_1):
         def QE(i):
             if not ok(i):
                 return
-            ec = work.tile([P, CH], U32, name="ec", tag="ec", align_bytes=64)
-            es = work.tile([P, CH], U8, name="es", tag="es", align_bytes=64)
+            ec = work.tile([P, CH], U32, name="ec", tag="ec", align_bytes=64, bufs=NB["ec"])
+            es = work.tile([P, CH], U8, name="es", tag="es", align_bytes=64, bufs=NB["ec"])
             nc.vector.quantize_mx(out=ec[:].bitcast(FP8X4), scales=es[:], in_=st[("ge", i)][:].rearrange("p n t -> p (n t)"))
             st[("ec", i)] = (ec, es)
 
@@ -268,7 +276,7 @@ def tile_memorybank2d_pa_t_kernel(tc, x, memory, out_0, out_1):
                 return
             ec, es = st[("ec", i)]
             if ("osb", i) not in st:
-                st[("osb", i)] = opool.tile([P, 4, CH], F32, name="osb", tag="osb")
+                st[("osb", i)] = opool.tile([P, 4, CH], F32, name="osb", tag="osb", bufs=NB["osb"] + 1)
             rec = psum.tile([P, CH], F32, name="rec", tag="rec", bufs=2)
             nc.tensor.matmul_mx(
                 out=rec[:],
@@ -296,99 +304,113 @@ def tile_memorybank2d_pa_t_kernel(tc, x, memory, out_0, out_1):
                 out=out_0[b].rearrange("(cc p) h w -> p cc (h w)", p=P)[:, :, n0 : n0 + CH], in_=st[("osb", i)][:]
             )
 
-        def MN2(part):
-            if part == 0:
-                for t in range(4):
-                    nc.vector.tensor_scalar(
-                        out=mn[:, t, :], in0=mem[:, t, :], scalar1=rm[:, t : t + 1], scalar2=None, op0=ALU.mult
-                    )
-            elif part == 1:
-                nc.vector.tensor_copy(out=g2[:], in_=mn[:].rearrange("p t c -> p c t"))
-            elif part == 2:
-                nc.vector.quantize_mx(out=mn2c[:].bitcast(FP8X4), scales=mn2s[:], in_=g2[:].rearrange("p c t -> p (c t)"))
+        def MSQ():
+            for t in range(4):
+                nc.scalar.activation(out=junk[:], in_=mem[:, t, :], func=ACT.Square, accum_out=ssm[:, t : t + 1])
 
-        def stage_a(i):
-            for g in range(2):
-                TX(i, g)
-                SQ(i, g, 0)
-                SQ(i, g, 1)
-            R(i)
+        def RM():
+            rsqrt_clamped(rm[:], ssmc[:], ssm[:])
 
-        for t in range(4):
-            nc.scalar.activation(out=junk[:], in_=mem[:, t, :], func=ACT.Square, accum_out=ssm[:, t : t + 1])
-        rsqrt_clamped(rm[:], ssmc[:], ssm[:])
-        stage_a(0)
-        stage_a(1)
-        for t in range(4):
-            nc.vector.tensor_scalar(
-                out=mnj[:, t, :, :],
-                in0=mem[:, t, :].rearrange("p (q j) -> p j q", j=4),
-                scalar1=rm[:, t : t + 1],
-                scalar2=None,
-                op0=ALU.mult,
-            )
-        TB(0)
-        XR(0)
-        tms = []
-        for h in range(2):
+        def NJ():
+            for t in range(4):
+                nc.vector.tensor_scalar(
+                    out=mnj[:, t, :, :],
+                    in0=mem[:, t, :].rearrange("p (q j) -> p j q", j=4),
+                    scalar1=rm[:, t : t + 1],
+                    scalar2=None,
+                    op0=ALU.mult,
+                )
+
+        def TM(h):
             tm = psum.tile([P, 4, 256], BF16, name="tm", tag="sim", bufs=2)
             for j in range(4):
                 for tt in range(2):
                     nc.tensor.transpose(
                         out=tm[:, j, P * tt : P * tt + P], in_=mnj[:, 2 * h + tt, j, :], identity=ident_b[:]
                     )
-            tms.append(tm)
-        A5(0, 1)
-        A5(0, 0)
-        for h in range(2):
-            nc.scalar.copy(out=gm[:, 256 * h : 256 * h + 256, :], in_=tms[h][:].rearrange("p j s -> p s j"))
-        QF(0)
-        nc.vector.quantize_mx(out=mnTc[:].bitcast(FP8X4), scales=mnTs[:], in_=gm[:].rearrange("p s j -> p (s j)"))
+            st[("tm", h)] = tm
 
-        for s in range(2, NCH + 3):
-            M1(s - 2, 0)
-            MAX(s - 2, 0)
-            M1(s - 2, 1)
-            MAX(s - 2, 1)
+        def XM(h):
+            nc.scalar.copy(out=gm[:, 256 * h : 256 * h + 256, :], in_=st[("tm", h)][:].rearrange("p j s -> p s j"))
+
+        def QM():
+            nc.vector.quantize_mx(out=mnTc[:].bitcast(FP8X4), scales=mnTs[:], in_=gm[:].rearrange("p s j -> p (s j)"))
+
+        def N2a():
+            for t in range(4):
+                nc.vector.tensor_scalar(
+                    out=mn[:, t, :], in0=mem[:, t, :], scalar1=rm[:, t : t + 1], scalar2=None, op0=ALU.mult
+                )
+
+        def N2b():
+            nc.vector.tensor_copy(out=g2[:], in_=mn[:].rearrange("p t c -> p c t"))
+
+        def N2c():
+            nc.vector.quantize_mx(out=mn2c[:].bitcast(FP8X4), scales=mn2s[:], in_=g2[:].rearrange("p c t -> p (c t)"))
+
+        for s in range(NCH + 6):
+            if s == 5:
+                N2b()
+            M1(s - 4, 0)
+            if s == 3:
+                TM(0)
+            M1(s - 4, 1)
+            TB(s - 2)
+            A5(s - 3, 1)
+            QE(s - 6)
+            MAX(s - 4, 0)
+            EXP(s - 4, 0)
+            if s == 0:
+                MSQ()
+            M2(s - 6, 2)
             TX(s, 0)
-            EXP(s - 2, 0)
-            TB(s - 1)
-            QE(s - 3)
-            EXP(s - 2, 1)
-            M1(s - 2, 2)
+            M1(s - 4, 3)
+            if s == 2:
+                TM(1)
+            MAX(s - 4, 1)
+            if s == 5:
+                N2c()
+            R(s - 1)
+            XR(s - 2)
+            if s == 3:
+                XM(0)
+            EXP(s - 4, 1)
+            QF(s - 3)
+            M1(s - 4, 2)
+            if s == 0:
+                RM()
+            MAX(s - 4, 3)
             SQ(s, 0, 0)
-            M2(s - 3, 1)
-            TE(s - 2, 0)
-            M1(s - 2, 3)
-            A5(s - 1, 0)
+            A5(s - 2, 3)
+            TE(s - 4, 0)
             SQ(s, 0, 1)
-            MAX(s - 2, 2)
-            M2(s - 3, 0)
-            XE(s - 2, 0)
-            EXP(s - 2, 2)
-            D(s - 3, 1)
-            if s == 2:
-                MN2(0)
-            MAX(s - 2, 3)
+            MAX(s - 4, 2)
+            D(s - 6, 2)
+            if s == 3:
+                QM()
+            EXP(s - 4, 3)
+            M2(s - 6, 0)
+            A5(s - 2, 2)
+            D(s - 6, 0)
+            M2(s - 6, 3)
             TX(s, 1)
-            D(s - 3, 0)
+            EXP(s - 4, 2)
+            RZ(s - 4)
+            D(s - 6, 3)
+            if s == 0:
+                N2a()
             if s == 2:
-                MN2(1)
-            A5(s - 1, 1)
-            EXP(s - 2, 3)
-            M2(s - 3, 2)
-            TE(s - 2, 1)
-            RZ(s - 2)
-            SQ(s, 1, 1)
-            M2(s - 3, 3)
-            QF(s - 1)
-            D(s - 3, 2)
-            if s == 2:
-                MN2(2)
+                XM(1)
+            XE(s - 4, 0)
+            if s == 1:
+                NJ()
+            M2(s - 6, 1)
+            TZ(s - 4)
+            D(s - 6, 1)
+            STORE(s - 6)
             SQ(s, 1, 0)
-            XE(s - 2, 1)
-            D(s - 3, 3)
-            STORE(s - 3)
-            R(s)
-            TZ(s - 2)
-            XZ(s - 2)
+            SQ(s, 1, 1)
+            TE(s - 4, 1)
+            A5(s - 2, 0)
+            XZ(s - 4)
+            XE(s - 4, 1)

@@ -259,7 +259,7 @@ def tile_memorybank2d_pa_t_kernel(tc, x, memory, out_0, out_1):
                 return
             b, n0 = where(i)
             rzb = work.tile([P, CH], F32, name="rzb", tag="rzb", bufs=NB["rzb"])
-            nc.scalar.copy(out=rzb[:], in_=st[("rzp", i)][:].rearrange("p k n -> p (k n)"))
+            nc.vector.tensor_copy(out=rzb[:], in_=st[("rzp", i)][:].rearrange("p k n -> p (k n)"))
             nc.sync.dma_start(out=out_1.rearrange("b h w -> b (h w)")[b : b + 1, n0 : n0 + CH], in_=rzb[0:1, :])
             st[("rzb", i)] = rzb
 
@@ -349,68 +349,68 @@ def tile_memorybank2d_pa_t_kernel(tc, x, memory, out_0, out_1):
             nc.vector.quantize_mx(out=mn2c[:].bitcast(FP8X4), scales=mn2s[:], in_=g2[:].rearrange("p c t -> p (c t)"))
 
         for s in range(NCH + 6):
-            if s == 5:
-                N2b()
             M1(s - 4, 0)
             if s == 3:
                 TM(0)
             M1(s - 4, 1)
             TB(s - 2)
-            A5(s - 3, 1)
             QE(s - 6)
+            A5(s - 3, 1)
             MAX(s - 4, 0)
             EXP(s - 4, 0)
+            M2(s - 6, 2)
+            MAX(s - 4, 1)
+            TX(s, 0)
+            XR(s - 2)
             if s == 0:
                 MSQ()
-            M2(s - 6, 2)
-            TX(s, 0)
-            M1(s - 4, 3)
-            if s == 2:
-                TM(1)
-            MAX(s - 4, 1)
-            if s == 5:
-                N2c()
-            R(s - 1)
-            XR(s - 2)
-            if s == 3:
-                XM(0)
             EXP(s - 4, 1)
-            QF(s - 3)
+            M1(s - 4, 3)
             M1(s - 4, 2)
+            QF(s - 3)
             if s == 0:
                 RM()
+            if s == 3:
+                XM(0)
             MAX(s - 4, 3)
-            SQ(s, 0, 0)
-            A5(s - 2, 3)
-            TE(s - 4, 0)
+            R(s - 1)
             SQ(s, 0, 1)
+            TE(s - 4, 0)
+            A5(s - 2, 3)
+            SQ(s, 0, 0)
+            EXP(s - 4, 3)
             MAX(s - 4, 2)
             D(s - 6, 2)
             if s == 3:
                 QM()
-            EXP(s - 4, 3)
-            M2(s - 6, 0)
             A5(s - 2, 2)
+            M2(s - 6, 0)
+            A5(s - 2, 0)
             D(s - 6, 0)
-            M2(s - 6, 3)
+            if s == 2:
+                TM(1)
             TX(s, 1)
+            M2(s - 6, 3)
+            if s == 5:
+                N2b()
             EXP(s - 4, 2)
             RZ(s - 4)
-            D(s - 6, 3)
-            if s == 0:
-                N2a()
             if s == 2:
                 XM(1)
             XE(s - 4, 0)
-            if s == 1:
-                NJ()
             M2(s - 6, 1)
+            D(s - 6, 3)
             TZ(s - 4)
+            if s == 5:
+                N2c()
+            SQ(s, 1, 0)
             D(s - 6, 1)
             STORE(s - 6)
-            SQ(s, 1, 0)
             SQ(s, 1, 1)
+            if s == 0:
+                N2a()
             TE(s - 4, 1)
-            A5(s - 2, 0)
+            if s == 1:
+                NJ()
             XZ(s - 4)
             XE(s - 4, 1)

@@ -21,7 +21,7 @@ FLOPS = 2 * 2 * B * HW * C * K
 ETG = False
 GP = (1, 2, 3)
 PIN = True
-NB = {"ss": 3, "r": 3, "gx": 3, "fn": 3, "e": 2, "ge": 4, "rz": 2, "rzb": 4, "ec": 2, "osb": 2, "rbs": 3}
+NB = {"ss": 3, "r": 3, "gx": 3, "fn": 3, "e": 3, "ge": 3, "rz": 2, "rzb": 4, "ec": 3, "osb": 2, "rbs": 3}
 
 
 def tile_memorybank2d_pa_t_kernel(tc, x, memory, out_0, out_1):
@@ -348,69 +348,69 @@ def tile_memorybank2d_pa_t_kernel(tc, x, memory, out_0, out_1):
         def N2c():
             nc.vector.quantize_mx(out=mn2c[:].bitcast(FP8X4), scales=mn2s[:], in_=g2[:].rearrange("p c t -> p (c t)"))
 
-        for s in range(NCH + 6):
+        for s in range(NCH + 7):
+            RZ(s - 5)
+            A5(s - 3, 2)
             M1(s - 4, 0)
-            if s == 3:
-                TM(0)
-            M1(s - 4, 1)
-            TB(s - 2)
-            QE(s - 6)
-            A5(s - 3, 1)
-            MAX(s - 4, 0)
-            EXP(s - 4, 0)
-            M2(s - 6, 2)
-            MAX(s - 4, 1)
-            TX(s, 0)
-            XR(s - 2)
-            if s == 0:
-                MSQ()
-            EXP(s - 4, 1)
-            M1(s - 4, 3)
-            M1(s - 4, 2)
-            QF(s - 3)
-            if s == 0:
-                RM()
-            if s == 3:
-                XM(0)
-            MAX(s - 4, 3)
-            R(s - 1)
-            SQ(s, 0, 1)
-            TE(s - 4, 0)
-            A5(s - 2, 3)
-            SQ(s, 0, 0)
-            EXP(s - 4, 3)
-            MAX(s - 4, 2)
-            D(s - 6, 2)
+            if s == 6:
+                N2c()
             if s == 3:
                 QM()
-            A5(s - 2, 2)
-            M2(s - 6, 0)
-            A5(s - 2, 0)
-            D(s - 6, 0)
-            if s == 2:
+            M1(s - 4, 1)
+            M2(s - 7, 2)
+            MAX(s - 4, 0)
+            TB(s - 2)
+            if s == 0:
+                MSQ()
+            EXP(s - 4, 0)
+            MAX(s - 4, 1)
+            D(s - 7, 2)
+            M2(s - 7, 0)
+            TX(s, 0)
+            if s == 0:
+                RM()
+            TE(s - 5, 0)
+            EXP(s - 4, 1)
+            M1(s - 4, 3)
+            QE(s - 6)
+            XR(s - 2)
+            SQ(s, 0, 0)
+            SQ(s, 0, 1)
+            QF(s - 3)
+            R(s - 1)
+            D(s - 7, 0)
+            XE(s - 5, 0)
+            if s == 1:
                 TM(1)
-            TX(s, 1)
-            M2(s - 6, 3)
-            if s == 5:
-                N2b()
-            EXP(s - 4, 2)
-            RZ(s - 4)
+            M1(s - 4, 2)
+            TZ(s - 5)
+            MAX(s - 4, 3)
+            if s == 1:
+                N2a()
+            M2(s - 7, 1)
+            A5(s - 2, 1)
+            MAX(s - 4, 2)
+            M2(s - 7, 3)
             if s == 2:
-                XM(1)
-            XE(s - 4, 0)
-            M2(s - 6, 1)
-            D(s - 6, 3)
-            TZ(s - 4)
-            if s == 5:
-                N2c()
-            SQ(s, 1, 0)
-            D(s - 6, 1)
-            STORE(s - 6)
+                XM(0)
+            EXP(s - 4, 3)
+            EXP(s - 4, 2)
+            if s == 1:
+                TM(0)
+            TX(s, 1)
+            A5(s - 2, 0)
+            if s == 3:
+                N2b()
+            D(s - 7, 1)
             SQ(s, 1, 1)
             if s == 0:
-                N2a()
-            TE(s - 4, 1)
-            if s == 1:
                 NJ()
-            XZ(s - 4)
-            XE(s - 4, 1)
+            TE(s - 5, 1)
+            SQ(s, 1, 0)
+            XZ(s - 5)
+            A5(s - 2, 3)
+            if s == 1:
+                XM(1)
+            D(s - 7, 3)
+            STORE(s - 7)
+            XE(s - 5, 1)

@@ -21,7 +21,13 @@ FLOPS = 2 * 2 * B * HW * C * K
 ETG = False
 GP = (1, 2, 3)
 PIN = True
-NB = {"ss": 3, "r": 3, "gx": 3, "fn": 3, "e": 3, "ge": 3, "rz": 2, "rzb": 4, "ec": 3, "osb": 2, "rbs": 3}
+GR_ = (3, 16)
+XZV = (0, 8)
+XRS = (11, 11)
+XE0V = (9, 2)
+XE1V = (16, 12)
+XTALT = 6
+NB = {"ss": 3, "r": 3, "gx": 3, "fn": 5, "e": 3, "ge": 3, "rz": 2, "rzb": 4, "ec": 3, "osb": 2, "rbs": 3}
 
 
 def tile_memorybank2d_pa_t_kernel(tc, x, memory, out_0, out_1):
@@ -74,6 +80,15 @@ def tile_memorybank2d_pa_t_kernel(tc, x, memory, out_0, out_1):
         def ok(i):
             return 0 <= i < NCH
 
+        def within(rng, i):
+            return rng[0] <= i < rng[1]
+
+        def copy_out(on_vector, out, in_):
+            if on_vector:
+                nc.vector.tensor_copy(out=out, in_=in_)
+            else:
+                nc.scalar.copy(out=out, in_=in_)
+
         def where(i):
             return i // (HW // CH), (i % (HW // CH)) * CH
 
@@ -91,7 +106,8 @@ def tile_memorybank2d_pa_t_kernel(tc, x, memory, out_0, out_1):
             x_sb, c0 = xchunk(i)
             if g == 0:
                 st[("ss", i)] = small.tile([P, 4], F32, name="ss", tag="ss", bufs=NB["ss"])
-            xt = psum.tile([P, 4, P], F32, name="xt", tag="xt", bufs=1)
+            alt = i < XTALT
+            xt = psum.tile([P, 4, P], F32, name="xt", tag=("rec" if alt else "xt"), bufs=(2 if alt else 1))
             w0 = c0 // 2 + P * g
             for j in range(4):
                 nc.tensor.transpose(out=xt[:, j, :], in_=x_sb[:].bitcast(F32)[:, j, w0 : w0 + P], identity=ident_f[:])
@@ -129,12 +145,13 @@ def tile_memorybank2d_pa_t_kernel(tc, x, memory, out_0, out_1):
             st[("gx", i)] = work.tile([P, CH, 4], BF16, name="gx", tag="gx", align_bytes=64, bufs=NB["gx"])
 
         def XR(i):
-            if not (ok(i) and len(GP) > 0):
+            if not (ok(i) and within(GR_, i)):
                 return
             rbs = work.tile([P, CH], F32, name="rbs", tag="rbs", bufs=NB["rbs"])
-            nc.vector.tensor_copy(
-                out=rbs[:].rearrange("p (g q e) -> p g q e", g=2, e=2),
-                in_=st[("rb", i)][:].rearrange("p (g e) q -> p g q e", e=2),
+            copy_out(
+                not within(XRS, i),
+                rbs[:].rearrange("p (g q e) -> p g q e", g=2, e=2),
+                st[("rb", i)][:].rearrange("p (g e) q -> p g q e", e=2),
             )
             st[("rbs", i)] = rbs
 
@@ -144,7 +161,7 @@ def tile_memorybank2d_pa_t_kernel(tc, x, memory, out_0, out_1):
             x_sb, c0 = xchunk(i)
             gx = st[("gx", i)]
             lo = P * k
-            if k in GP:
+            if k in GP and within(GR_, i):
                 nc.gpsimd.tensor_tensor(
                     out=gx[:, lo : lo + P, :],
                     in0=st[("rbs", i)][:, lo : lo + P].unsqueeze(2).to_broadcast([P, P, 4]),
@@ -236,7 +253,7 @@ def tile_memorybank2d_pa_t_kernel(tc, x, memory, out_0, out_1):
                     out=dst, in0=ets[:].rearrange("p t n -> p n t"), scalar1=1.0, scalar2=0.0, op0=ALU.mult, op1=ALU.add
                 )
             else:
-                nc.scalar.copy(out=dst, in_=et[:].rearrange("p t n -> p n t"))
+                copy_out(within(XE1V if h else XE0V, i), dst, et[:].rearrange("p t n -> p n t"))
 
         def RZ(i):
             if not ok(i):
@@ -259,7 +276,7 @@ def tile_memorybank2d_pa_t_kernel(tc, x, memory, out_0, out_1):
                 return
             b, n0 = where(i)
             rzb = work.tile([P, CH], F32, name="rzb", tag="rzb", bufs=NB["rzb"])
-            nc.vector.tensor_copy(out=rzb[:], in_=st[("rzp", i)][:].rearrange("p k n -> p (k n)"))
+            copy_out(within(XZV, i), rzb[:], st[("rzp", i)][:].rearrange("p k n -> p (k n)"))
             nc.sync.dma_start(out=out_1.rearrange("b h w -> b (h w)")[b : b + 1, n0 : n0 + CH], in_=rzb[0:1, :])
             st[("rzb", i)] = rzb
 
@@ -348,69 +365,69 @@ def tile_memorybank2d_pa_t_kernel(tc, x, memory, out_0, out_1):
         def N2c():
             nc.vector.quantize_mx(out=mn2c[:].bitcast(FP8X4), scales=mn2s[:], in_=g2[:].rearrange("p c t -> p (c t)"))
 
-        for s in range(NCH + 7):
-            RZ(s - 5)
-            A5(s - 3, 2)
-            M1(s - 4, 0)
-            if s == 6:
-                N2c()
-            if s == 3:
-                QM()
-            M1(s - 4, 1)
-            M2(s - 7, 2)
-            MAX(s - 4, 0)
-            TB(s - 2)
+        for s in range(NCH + 9):
             if s == 0:
                 MSQ()
-            EXP(s - 4, 0)
-            MAX(s - 4, 1)
-            D(s - 7, 2)
-            M2(s - 7, 0)
-            TX(s, 0)
-            if s == 0:
-                RM()
-            TE(s - 5, 0)
-            EXP(s - 4, 1)
-            M1(s - 4, 3)
-            QE(s - 6)
-            XR(s - 2)
-            SQ(s, 0, 0)
-            SQ(s, 0, 1)
-            QF(s - 3)
-            R(s - 1)
-            D(s - 7, 0)
-            XE(s - 5, 0)
-            if s == 1:
-                TM(1)
-            M1(s - 4, 2)
-            TZ(s - 5)
-            MAX(s - 4, 3)
+            if s == 4:
+                XM(1)
+            M1(s - 6, 0)
+            MAX(s - 6, 0)
+            EXP(s - 6, 0)
+            M1(s - 6, 1)
+            M2(s - 9, 2)
+            MAX(s - 6, 1)
+            TB(s - 2)
             if s == 1:
                 N2a()
-            M2(s - 7, 1)
-            A5(s - 2, 1)
-            MAX(s - 4, 2)
-            M2(s - 7, 3)
+            RZ(s - 7)
+            M2(s - 9, 0)
+            TX(s, 0)
+            EXP(s - 6, 1)
+            if s == 5:
+                QM()
+            if s == 0:
+                RM()
+            D(s - 9, 2)
+            SQ(s, 0, 0)
+            TE(s - 7, 0)
+            M1(s - 6, 3)
+            A5(s - 3, 3)
             if s == 2:
-                XM(0)
-            EXP(s - 4, 3)
-            EXP(s - 4, 2)
-            if s == 1:
                 TM(0)
-            TX(s, 1)
-            A5(s - 2, 0)
-            if s == 3:
+            M2(s - 9, 1)
+            if s == 2:
                 N2b()
-            D(s - 7, 1)
-            SQ(s, 1, 1)
+            D(s - 9, 0)
+            M1(s - 6, 2)
+            QE(s - 8)
+            A5(s - 3, 1)
+            A5(s - 2, 0)
+            MAX(s - 6, 3)
+            M2(s - 9, 3)
+            SQ(s, 0, 1)
+            if s == 3:
+                N2c()
+            TX(s, 1)
+            XE(s - 7, 0)
+            TZ(s - 7)
+            if s == 3:
+                TM(1)
+            if s == 3:
+                XM(0)
+            MAX(s - 6, 2)
+            EXP(s - 6, 3)
+            XR(s - 2)
             if s == 0:
                 NJ()
-            TE(s - 5, 1)
+            TE(s - 7, 1)
+            EXP(s - 6, 2)
             SQ(s, 1, 0)
-            XZ(s - 5)
-            A5(s - 2, 3)
-            if s == 1:
-                XM(1)
-            D(s - 7, 3)
-            STORE(s - 7)
-            XE(s - 5, 1)
+            SQ(s, 1, 1)
+            QF(s - 3)
+            XE(s - 7, 1)
+            R(s - 1)
+            XZ(s - 7)
+            D(s - 9, 1)
+            A5(s - 2, 2)
+            D(s - 9, 3)
+            STORE(s - 9)

@@ -16,18 +16,18 @@ P = 128
 B, C, HW, K = 2, 512, 4096, 512
 CH = 512
 NCH = B * HW // CH
-LOADPX = 1024
+LOADS = (512, 512) + (1024,) * 7
 FLOPS = 2 * 2 * B * HW * C * K
 ETG = False
 GP = (1, 2, 3)
 PIN = True
-GR_ = (3, 16)
-XZV = (0, 8)
-XRS = (11, 11)
-XE0V = (9, 2)
-XE1V = (16, 12)
-XTALT = 6
-NB = {"ss": 3, "r": 3, "gx": 3, "fn": 5, "e": 3, "ge": 3, "rz": 2, "rzb": 4, "ec": 3, "osb": 2, "rbs": 3}
+GR_ = (2, 16)
+XZV = (12, 12)
+XRS = (0, 16)
+XE0V = (14, 14)
+XE1V = (15, 11)
+XTALT = 7
+NB = {"ss": 3, "r": 3, "gx": 4, "fn": 3, "e": 3, "ge": 3, "rz": 2, "rzb": 4, "ec": 3, "osb": 2, "rbs": 3}
 
 
 def tile_memorybank2d_pa_t_kernel(tc, x, memory, out_0, out_1):
@@ -43,17 +43,17 @@ def tile_memorybank2d_pa_t_kernel(tc, x, memory, out_0, out_1):
             ctx.enter_context(tc.manual_schedule())
 
         mem = const.tile([P, 4, C], BF16, name="mem")
-        nc.sync.dma_start(out=mem[:], in_=memory.rearrange("(p t) c -> p t c", t=4))
-        xs = []
-        for ld in range(B * HW // LOADPX):
-            b = ld // (HW // LOADPX)
-            n0 = (ld % (HW // LOADPX)) * LOADPX
-            x_sb = xpool.tile([P, 4, LOADPX], BF16, name="x%d" % ld)
+        xloc = []
+        for ld, width in enumerate(LOADS):
+            first = len(xloc) * CH
+            b, n0 = first // HW, first % HW
+            x_sb = xpool.tile([P, 4, width], BF16, name="x%d" % ld)
             nc.sync.dma_start(
-                out=x_sb[:],
-                in_=x[b].rearrange("(p j) h w -> p j (h w)", j=4)[:, :, n0 : n0 + LOADPX],
+                out=x_sb[:], in_=x[b].rearrange("(p j) h w -> p j (h w)", j=4)[:, :, n0 : n0 + width]
             )
-            xs.append(x_sb)
+            xloc.extend([(x_sb, c0) for c0 in range(0, width, CH)])
+            if ld == 0:
+                nc.sync.dma_start(out=mem[:], in_=memory.rearrange("(p t) c -> p t c", t=4))
 
         ident_f = const.tile([P, P], F32, name="ident_f")
         make_identity(nc, ident_f[:])
@@ -62,6 +62,7 @@ def tile_memorybank2d_pa_t_kernel(tc, x, memory, out_0, out_1):
         neghalf = const.tile([P, 4], F32, name="neghalf")
         nc.vector.memset(neghalf[:], -0.5)
         junk = const.tile([P, 512], BF16, name="junk")
+        junkv = const.tile([P, P], F32, name="junkv")
 
         mn = const.tile([P, 4, C], BF16, name="mn")
         mnj = const.tile([P, 4, 4, P], BF16, name="mnj")
@@ -93,45 +94,67 @@ def tile_memorybank2d_pa_t_kernel(tc, x, memory, out_0, out_1):
             return i // (HW // CH), (i % (HW // CH)) * CH
 
         def xchunk(i):
-            per = LOADPX // CH
-            return xs[i // per], (i % per) * CH
+            return xloc[i]
 
         def rsqrt_clamped(out, tmp, ss):
             nc.gpsimd.tensor_scalar(out=tmp, in0=ss, scalar1=1e-24, scalar2=None, op0=ALU.max)
             nc.gpsimd.tensor_tensor(out=out, in0=tmp, in1=neghalf[:], op=ALU.pow)
 
-        def TX(i, g):
+        def GR(i):
             if not ok(i):
                 return
             x_sb, c0 = xchunk(i)
-            if g == 0:
-                st[("ss", i)] = small.tile([P, 4], F32, name="ss", tag="ss", bufs=NB["ss"])
+            st[("ssv", i)] = small.tile([P, 3], F32, name="ssv", tag="ssv", bufs=NB["ss"])
             alt = i < XTALT
-            xt = psum.tile([P, 4, P], F32, name="xt", tag=("rec" if alt else "xt"), bufs=(2 if alt else 1))
-            w0 = c0 // 2 + P * g
-            for j in range(4):
-                nc.tensor.transpose(out=xt[:, j, :], in_=x_sb[:].bitcast(F32)[:, j, w0 : w0 + P], identity=ident_f[:])
-            st[("xt", i, g)] = xt
+            gr = psum.tile([P, 3, P], F32, name="gr", tag=("rec" if alt else "xt"), bufs=(2 if alt else 1))
+            for k in range(3):
+                for j in range(4):
+                    blk = x_sb[:, j, c0 + P * k : c0 + P * k + P]
+                    nc.tensor.matmul(out=gr[:, k, :], lhsT=blk, rhs=blk, start=(j == 0), stop=(j == 3))
+            st[("gr", i)] = gr
 
-        def SQ(i, g, e):
+        def DG(i, k):
             if not ok(i):
                 return
-            xt = st[("xt", i, g)]
-            ss = st[("ss", i)]
-            xv = xt[:].bitcast(BF16).rearrange("p j (q e) -> p j q e", e=2)
+            nc.vector.scalar_tensor_tensor(
+                out=junkv[:],
+                in0=st[("gr", i)][:, k, :],
+                scalar=1.0,
+                in1=ident_f[:],
+                op0=ALU.mult,
+                op1=ALU.mult,
+                accum_out=st[("ssv", i)][:, k : k + 1],
+            )
+
+        def TX(i):
+            if not ok(i):
+                return
+            x_sb, c0 = xchunk(i)
+            st[("sss", i)] = small.tile([P, 1], F32, name="sss", tag="sss", bufs=NB["ss"])
+            alt = i < XTALT
+            xt = psum.tile([P, 4, P], BF16, name="xt", tag=("rec" if alt else "xt"), bufs=(2 if alt else 1))
+            for j in range(4):
+                nc.tensor.transpose(out=xt[:, j, :], in_=x_sb[:, j, c0 + 3 * P : c0 + 4 * P], identity=ident_b[:])
+            st[("xt", i)] = xt
+
+        def SQ(i):
+            if not ok(i):
+                return
             nc.scalar.activation(
                 out=junk[:].rearrange("p (j q) -> p j q", j=4),
-                in_=xv[:, :, :, e],
+                in_=st[("xt", i)][:],
                 func=ACT.Square,
-                accum_out=ss[:, 2 * g + e : 2 * g + e + 1],
+                accum_out=st[("sss", i)][:],
             )
 
         def R(i):
             if not ok(i):
                 return
-            ssc = small.tile([P, 4], F32, name="ssc", tag="ssc", bufs=NB["r"])
+            rr = small.tile([P, 4], F32, name="rr", tag="rr", bufs=NB["r"])
             r = small.tile([P, 4], F32, name="r", tag="r", bufs=NB["r"])
-            rsqrt_clamped(r[:], ssc[:], st[("ss", i)][:])
+            nc.gpsimd.tensor_tensor(out=rr[:, 0:3], in0=st[("ssv", i)][:], in1=neghalf[:, 0:3], op=ALU.pow)
+            nc.gpsimd.tensor_tensor(out=rr[:, 3:4], in0=st[("sss", i)][:], in1=neghalf[:, 3:4], op=ALU.pow)
+            nc.gpsimd.tensor_scalar(out=r[:], in0=rr[:], scalar1=1e12, scalar2=0.0, op0=ALU.min, op1=ALU.max)
             st[("r", i)] = r
 
         def TB(i):
@@ -148,35 +171,22 @@ def tile_memorybank2d_pa_t_kernel(tc, x, memory, out_0, out_1):
             if not (ok(i) and within(GR_, i)):
                 return
             rbs = work.tile([P, CH], F32, name="rbs", tag="rbs", bufs=NB["rbs"])
-            copy_out(
-                not within(XRS, i),
-                rbs[:].rearrange("p (g q e) -> p g q e", g=2, e=2),
-                st[("rb", i)][:].rearrange("p (g e) q -> p g q e", e=2),
-            )
+            copy_out(not within(XRS, i), rbs[:], st[("rb", i)][:].rearrange("p k n -> p (k n)"))
             st[("rbs", i)] = rbs
 
         def A5(i, k):
             if not ok(i):
                 return
             x_sb, c0 = xchunk(i)
-            gx = st[("gx", i)]
             lo = P * k
             if k in GP and within(GR_, i):
-                nc.gpsimd.tensor_tensor(
-                    out=gx[:, lo : lo + P, :],
-                    in0=st[("rbs", i)][:, lo : lo + P].unsqueeze(2).to_broadcast([P, P, 4]),
-                    in1=x_sb[:, :, c0 + lo : c0 + lo + P].rearrange("p j n -> p n j"),
-                    op=ALU.mult,
-                )
-                return
-            g, q0 = k // 2, 64 * (k % 2)
-            nc.vector.tensor_tensor(
-                out=gx[:, lo : lo + P, :].rearrange("p (q e) j -> p q e j", e=2),
-                in0=st[("rb", i)][:, 2 * g : 2 * g + 2, q0 : q0 + 64]
-                .rearrange("p e q -> p q e")
-                .unsqueeze(3)
-                .to_broadcast([P, 64, 2, 4]),
-                in1=x_sb[:, :, c0 + lo : c0 + lo + P].rearrange("p j (q e) -> p q e j", e=2),
+                eng, rsrc = nc.gpsimd, st[("rbs", i)][:, lo : lo + P]
+            else:
+                eng, rsrc = nc.vector, st[("rb", i)][:, k, :]
+            eng.tensor_tensor(
+                out=st[("gx", i)][:, lo : lo + P, :],
+                in0=rsrc.unsqueeze(2).to_broadcast([P, P, 4]),
+                in1=x_sb[:, :, c0 + lo : c0 + lo + P].rearrange("p j n -> p n j"),
                 op=ALU.mult,
             )
 
@@ -187,7 +197,6 @@ def tile_memorybank2d_pa_t_kernel(tc, x, memory, out_0, out_1):
             fns = work.tile([P, CH], U8, name="fns", tag="fns", align_bytes=64, bufs=NB["fn"])
             nc.vector.quantize_mx(out=fnc[:].bitcast(FP8X4), scales=fns[:], in_=st[("gx", i)][:].rearrange("p n j -> p (n j)"))
             st[("fn", i)] = (fnc, fns)
-
         def M1(i, k):
             if not ok(i):
                 return
@@ -312,13 +321,9 @@ def tile_memorybank2d_pa_t_kernel(tc, x, memory, out_0, out_1):
             nc.vector.tensor_tensor(
                 out=st[("osb", i)][:, cc, :], in0=st[("rec", i, cc)][:], in1=st[("rzb", i)][:], op=ALU.mult
             )
-
-        def STORE(i):
-            if not ok(i):
-                return
             b, n0 = where(i)
             nc.sync.dma_start(
-                out=out_0[b].rearrange("(cc p) h w -> p cc (h w)", p=P)[:, :, n0 : n0 + CH], in_=st[("osb", i)][:]
+                out=out_0[b].rearrange("(cc p) h w -> p cc (h w)", p=P)[:, cc, n0 : n0 + CH], in_=st[("osb", i)][:, cc, :]
             )
 
         def MSQ():
@@ -330,12 +335,11 @@ def tile_memorybank2d_pa_t_kernel(tc, x, memory, out_0, out_1):
 
         def NJ():
             for t in range(4):
-                nc.vector.tensor_scalar(
+                nc.scalar.activation(
                     out=mnj[:, t, :, :],
-                    in0=mem[:, t, :].rearrange("p (q j) -> p j q", j=4),
-                    scalar1=rm[:, t : t + 1],
-                    scalar2=None,
-                    op0=ALU.mult,
+                    in_=mem[:, t, :].rearrange("p (q j) -> p j q", j=4),
+                    func=ACT.Copy,
+                    scale=rm[:, t : t + 1],
                 )
 
         def TM(h):
@@ -355,79 +359,76 @@ def tile_memorybank2d_pa_t_kernel(tc, x, memory, out_0, out_1):
 
         def N2a():
             for t in range(4):
-                nc.vector.tensor_scalar(
-                    out=mn[:, t, :], in0=mem[:, t, :], scalar1=rm[:, t : t + 1], scalar2=None, op0=ALU.mult
-                )
+                nc.scalar.activation(out=mn[:, t, :], in_=mem[:, t, :], func=ACT.Copy, scale=rm[:, t : t + 1])
 
         def N2b():
-            nc.vector.tensor_copy(out=g2[:], in_=mn[:].rearrange("p t c -> p c t"))
+            nc.scalar.copy(out=g2[:], in_=mn[:].rearrange("p t c -> p c t"))
 
         def N2c():
             nc.vector.quantize_mx(out=mn2c[:].bitcast(FP8X4), scales=mn2s[:], in_=g2[:].rearrange("p c t -> p (c t)"))
 
-        for s in range(NCH + 9):
+        for s in range(NCH + 8):
+            M1(s - 5, 0)
+            if s == 5:
+                N2b()
+            if s == 1:
+                RM()
+            MAX(s - 5, 0)
+            EXP(s - 5, 0)
+            M2(s - 8, 0)
+            M1(s - 5, 1)
+            D(s - 8, 0)
+            M2(s - 8, 2)
+            GR(s)
+            A5(s - 3, 1)
+            if s == 1:
+                NJ()
+            if s == 4:
+                QM()
+            MAX(s - 5, 1)
+            QF(s - 4)
+            TB(s - 2)
+            D(s - 8, 2)
+            TE(s - 6, 0)
+            M1(s - 5, 3)
+            M2(s - 8, 1)
+            RZ(s - 6)
+            EXP(s - 5, 1)
+            R(s - 1)
             if s == 0:
                 MSQ()
-            if s == 4:
-                XM(1)
-            M1(s - 6, 0)
-            MAX(s - 6, 0)
-            EXP(s - 6, 0)
-            M1(s - 6, 1)
-            M2(s - 9, 2)
-            MAX(s - 6, 1)
-            TB(s - 2)
-            if s == 1:
-                N2a()
-            RZ(s - 7)
-            M2(s - 9, 0)
-            TX(s, 0)
-            EXP(s - 6, 1)
-            if s == 5:
-                QM()
-            if s == 0:
-                RM()
-            D(s - 9, 2)
-            SQ(s, 0, 0)
-            TE(s - 7, 0)
-            M1(s - 6, 3)
-            A5(s - 3, 3)
+            DG(s, 0)
+            M1(s - 5, 2)
+            TZ(s - 6)
             if s == 2:
-                TM(0)
-            M2(s - 9, 1)
-            if s == 2:
-                N2b()
-            D(s - 9, 0)
-            M1(s - 6, 2)
-            QE(s - 8)
-            A5(s - 3, 1)
-            A5(s - 2, 0)
-            MAX(s - 6, 3)
-            M2(s - 9, 3)
-            SQ(s, 0, 1)
-            if s == 3:
-                N2c()
-            TX(s, 1)
-            XE(s - 7, 0)
-            TZ(s - 7)
-            if s == 3:
                 TM(1)
+            DG(s, 2)
+            XE(s - 6, 0)
+            if s == 3:
+                XM(1)
+            DG(s, 1)
+            TX(s)
+            XR(s - 2)
+            MAX(s - 5, 3)
+            QE(s - 7)
+            EXP(s - 5, 3)
+            M2(s - 8, 3)
+            MAX(s - 5, 2)
+            XZ(s - 6)
+            TE(s - 6, 1)
+            if s == 2:
+                N2a()
+            if s == 6:
+                N2c()
+            EXP(s - 5, 2)
             if s == 3:
                 XM(0)
-            MAX(s - 6, 2)
-            EXP(s - 6, 3)
-            XR(s - 2)
-            if s == 0:
-                NJ()
-            TE(s - 7, 1)
-            EXP(s - 6, 2)
-            SQ(s, 1, 0)
-            SQ(s, 1, 1)
-            QF(s - 3)
-            XE(s - 7, 1)
-            R(s - 1)
-            XZ(s - 7)
-            D(s - 9, 1)
+            A5(s - 3, 3)
+            SQ(s)
+            XE(s - 6, 1)
+            D(s - 8, 1)
+            A5(s - 2, 0)
             A5(s - 2, 2)
-            D(s - 9, 3)
-            STORE(s - 9)
+            if s == 2:
+                TM(0)
+            D(s - 8, 3)

@@ -18,16 +18,25 @@ CH = 512
 NCH = B * HW // CH
 LOADS = (512, 512) + (1024,) * 7
 FLOPS = 2 * 2 * B * HW * C * K
-ETG = False
-GP = (1, 2, 3)
-PIN = True
-GR_ = (2, 16)
-XZV = (12, 12)
-XRS = (0, 16)
-XE0V = (14, 14)
-XE1V = (15, 11)
-XTALT = 7
-NB = {"ss": 3, "r": 3, "gx": 4, "fn": 3, "e": 3, "ge": 3, "rz": 2, "rzb": 4, "ec": 3, "osb": 2, "rbs": 3}
+LM2 = 10
+ZM2 = 7
+NZ = 3
+LSQ = -14
+LCL = -10
+LTB = -6
+LXR = -6
+LTZ = 5
+LRZ = 4
+LAV = -5
+LQE = 6
+LQF = -2
+LAG = -5
+NG = 4
+LTE = 2
+LXE = 2
+DO = (0, 1, 2, 3)
+TO = (0, 2)
+SO = (0, 1, 2, 3)
 
 
 def tile_memorybank2d_pa_t_kernel(tc, x, memory, out_0, out_1):
@@ -35,176 +44,229 @@ def tile_memorybank2d_pa_t_kernel(tc, x, memory, out_0, out_1):
     with ExitStack() as ctx:
         const = ctx.enter_context(tc.tile_pool(name="const", bufs=1))
         xpool = ctx.enter_context(tc.tile_pool(name="xpool", bufs=1))
-        small = ctx.enter_context(tc.tile_pool(name="small", bufs=4))
-        work = ctx.enter_context(tc.tile_pool(name="work", bufs=2))
+        small = ctx.enter_context(tc.tile_pool(name="small", bufs=3))
+        work = ctx.enter_context(tc.tile_pool(name="work", bufs=3))
         opool = ctx.enter_context(tc.tile_pool(name="opool", bufs=3))
         psum = ctx.enter_context(tc.psum_pool(name="psum", bufs=1))
-        if PIN:
-            ctx.enter_context(tc.manual_schedule())
+        ctx.enter_context(tc.manual_schedule())
 
         mem = const.tile([P, 4, C], BF16, name="mem")
+        nc.sync.dma_start(out=mem[:], in_=memory.rearrange("(p t) c -> p t c", t=4))
         xloc = []
         for ld, width in enumerate(LOADS):
             first = len(xloc) * CH
             b, n0 = first // HW, first % HW
             x_sb = xpool.tile([P, 4, width], BF16, name="x%d" % ld)
-            nc.sync.dma_start(
-                out=x_sb[:], in_=x[b].rearrange("(p j) h w -> p j (h w)", j=4)[:, :, n0 : n0 + width]
-            )
-            xloc.extend([(x_sb, c0) for c0 in range(0, width, CH)])
-            if ld == 0:
-                nc.sync.dma_start(out=mem[:], in_=memory.rearrange("(p t) c -> p t c", t=4))
+            src = x[b].rearrange("(p j) h w -> p j (h w)", j=4)
+            step = 256 if ld == 0 else width
+            for c0 in range(0, width, step):
+                nc.sync.dma_start(out=x_sb[:, :, c0 : c0 + step], in_=src[:, :, n0 + c0 : n0 + c0 + step])
+            words = x_sb[:].rearrange("p j n -> p (j n)").bitcast(F32)
+            xloc.extend([(x_sb, words, width // 2, c0) for c0 in range(0, width, CH)])
 
-        ident_f = const.tile([P, P], F32, name="ident_f")
-        make_identity(nc, ident_f[:])
-        ident_b = const.tile([P, P], BF16, name="ident_b")
-        make_identity(nc, ident_b[:])
         neghalf = const.tile([P, 4], F32, name="neghalf")
         nc.vector.memset(neghalf[:], -0.5)
+        ident = const.tile([P, P], F32, name="ident")
+        make_identity(nc, ident[:])
         junk = const.tile([P, 512], BF16, name="junk")
-        junkv = const.tile([P, P], F32, name="junkv")
+        junkf = const.tile([P, 512], F32, name="junkf")
+        dummy = const.tile([P, 1], F32, name="dummy")
+        one = const.tile([P, 1], F32, name="one")
+        nc.vector.memset(one[:], 1.0)
+        nc.scalar.activation(out=dummy[:], in_=one[:], func=ACT.Abs_reciprocal_sqrt)
 
         mn = const.tile([P, 4, C], BF16, name="mn")
-        mnj = const.tile([P, 4, 4, P], BF16, name="mnj")
         g2 = const.tile([P, C, 4], BF16, name="g2", align_bytes=64)
-        gm = const.tile([P, K, 4], BF16, name="gm", align_bytes=64)
+        gm = const.tile([P, K * 4], BF16, name="gm", align_bytes=64)
         mn2c = const.tile([P, C], U32, name="mn2c", align_bytes=64)
         mn2s = const.tile([P, C], U8, name="mn2s", align_bytes=64)
         mnTc = const.tile([P, K], U32, name="mnTc", align_bytes=64)
         mnTs = const.tile([P, K], U8, name="mnTs", align_bytes=64)
         ssm = const.tile([P, 4], F32, name="ssm")
-        ssmc = const.tile([P, 4], F32, name="ssmc")
-        rm = const.tile([P, 4], F32, name="rm")
+        rzw = [const.tile([P, P], F32, name="rzw%d" % n) for n in range(2)]
+        for n in range(2):
+            nc.gpsimd.memset(rzw[n][:], 0.0)
+        mn_words = mn[:].rearrange("p t c -> p (t c)").bitcast(F32)
 
         st = {}
+
+        def clamp(ss):
+            clamped = small.tile([P, 4], F32, name="clamped", tag="clamped")
+            nc.vector.tensor_scalar(out=clamped[:], in0=ss, scalar1=1e-24, scalar2=None, op0=ALU.max)
+            return clamped
+
+        def MSQS(t):
+            nc.scalar.activation(out=junk[:], in_=mem[:, t, :], func=ACT.Square, accum_out=ssm[:, t : t + 1])
+
+        def MSQV(t):
+            nc.vector.scalar_tensor_tensor(
+                out=junkf[:], in0=mem[:, t, :], scalar=1.0, in1=mem[:, t, :], op0=ALU.mult, op1=ALU.mult, accum_out=ssm[:, t : t + 1]
+            )
+
+        def CM():
+            st["cm"] = clamp(ssm[:])
+
+        def RM():
+            st["rm"] = const.tile([P, 4], F32, name="rm")
+            nc.scalar.activation(out=st["rm"][:], in_=st["cm"][:], func=ACT.Abs_reciprocal_sqrt)
+
+        def MN(t):
+            nc.vector.tensor_scalar(
+                out=mn[:, t, :], in0=mem[:, t, :], scalar1=st["rm"][:, t : t + 1], scalar2=None, op0=ALU.mult
+            )
+
+        def TM(u):
+            tm = psum.tile([P, 2, 2, P], F32, name="tm", tag="sim", bufs=2)
+            for e in range(2):
+                for v in range(2):
+                    first = (2 * u + e) * (C // 2) + v
+                    nc.tensor.transpose(out=tm[:, e, v, :], in_=mn_words[:, first : first + 255 : 2], identity=ident[:])
+            st[("tm", u)] = tm
+
+        def XM(u, eng):
+            dst = gm[:].bitcast(F32)[:, 512 * u : 512 * u + 512]
+            eng(out=dst.rearrange("p (q e v) -> p q e v", e=2, v=2), in_=st[("tm", u)][:].rearrange("p e v q -> p q e v"))
+
+        def QM():
+            nc.vector.quantize_mx(out=mnTc[:].bitcast(FP8X4), scales=mnTs[:], in_=gm[:])
+
+        def G2(h):
+            nc.gpsimd.tensor_scalar(
+                out=g2[:, 256 * h : 256 * h + 256, :],
+                in0=mn[:, :, 256 * h : 256 * h + 256].rearrange("p t c -> p c t"),
+                scalar1=1.0,
+                scalar2=0.0,
+                op0=ALU.mult,
+                op1=ALU.add,
+            )
+
+        def Q2():
+            nc.vector.quantize_mx(out=mn2c[:].bitcast(FP8X4), scales=mn2s[:], in_=g2[:].rearrange("p c t -> p (c t)"))
 
         def ok(i):
             return 0 <= i < NCH
 
-        def within(rng, i):
-            return rng[0] <= i < rng[1]
-
-        def copy_out(on_vector, out, in_):
-            if on_vector:
-                nc.vector.tensor_copy(out=out, in_=in_)
-            else:
-                nc.scalar.copy(out=out, in_=in_)
-
         def where(i):
             return i // (HW // CH), (i % (HW // CH)) * CH
 
-        def xchunk(i):
-            return xloc[i]
-
-        def rsqrt_clamped(out, tmp, ss):
-            nc.gpsimd.tensor_scalar(out=tmp, in0=ss, scalar1=1e-24, scalar2=None, op0=ALU.max)
-            nc.gpsimd.tensor_tensor(out=out, in0=tmp, in1=neghalf[:], op=ALU.pow)
-
         def GR(i):
-            if not ok(i):
-                return
-            x_sb, c0 = xchunk(i)
-            st[("ssv", i)] = small.tile([P, 3], F32, name="ssv", tag="ssv", bufs=NB["ss"])
-            alt = i < XTALT
-            gr = psum.tile([P, 3, P], F32, name="gr", tag=("rec" if alt else "xt"), bufs=(2 if alt else 1))
-            for k in range(3):
+            x_sb, words, wide, c0 = xloc[i]
+            gr = psum.tile([P, 4, P], F32, name="gr", tag="rec", bufs=2)
+            st[("ss", i)] = small.tile([P, 4], F32, name="ss", tag="ss")
+            for k in range(4):
                 for j in range(4):
                     blk = x_sb[:, j, c0 + P * k : c0 + P * k + P]
                     nc.tensor.matmul(out=gr[:, k, :], lhsT=blk, rhs=blk, start=(j == 0), stop=(j == 3))
             st[("gr", i)] = gr
 
         def DG(i, k):
-            if not ok(i):
-                return
             nc.vector.scalar_tensor_tensor(
-                out=junkv[:],
+                out=junkf[:, 0:P],
                 in0=st[("gr", i)][:, k, :],
                 scalar=1.0,
-                in1=ident_f[:],
+                in1=ident[:],
                 op0=ALU.mult,
                 op1=ALU.mult,
-                accum_out=st[("ssv", i)][:, k : k + 1],
+                accum_out=st[("ss", i)][:, k : k + 1],
             )
 
-        def TX(i):
-            if not ok(i):
-                return
-            x_sb, c0 = xchunk(i)
-            st[("sss", i)] = small.tile([P, 1], F32, name="sss", tag="sss", bufs=NB["ss"])
-            alt = i < XTALT
-            xt = psum.tile([P, 4, P], BF16, name="xt", tag=("rec" if alt else "xt"), bufs=(2 if alt else 1))
+        def TX(i, h):
+            x_sb, words, wide, c0 = xloc[i]
+            if h == 0:
+                st[("ss", i)] = small.tile([P, 4], F32, name="ss", tag="ss")
+            xt = psum.tile([P, 512], F32, name="xt", tag="xt", bufs=1)
             for j in range(4):
-                nc.tensor.transpose(out=xt[:, j, :], in_=x_sb[:, j, c0 + 3 * P : c0 + 4 * P], identity=ident_b[:])
-            st[("xt", i)] = xt
+                w0 = j * wide + c0 // 2 + P * h
+                nc.tensor.transpose(out=xt[:, P * j : P * j + P], in_=words[:, w0 : w0 + P], identity=ident[:])
+            st[("xt", i, h)] = xt
 
-        def SQ(i):
-            if not ok(i):
-                return
+        def SQ(i, h, e):
             nc.scalar.activation(
-                out=junk[:].rearrange("p (j q) -> p j q", j=4),
-                in_=st[("xt", i)][:],
+                out=junk[:],
+                in_=st[("xt", i, h)][:].bitcast(BF16).rearrange("p (m e) -> p e m", e=2)[:, e, :],
                 func=ACT.Square,
-                accum_out=st[("sss", i)][:],
+                accum_out=st[("ss", i)][:, 2 * h + e : 2 * h + e + 1],
             )
+
+        def CL(i):
+            st[("cl", i)] = clamp(st[("ss", i)][:])
 
         def R(i):
-            if not ok(i):
-                return
-            rr = small.tile([P, 4], F32, name="rr", tag="rr", bufs=NB["r"])
-            r = small.tile([P, 4], F32, name="r", tag="r", bufs=NB["r"])
-            nc.gpsimd.tensor_tensor(out=rr[:, 0:3], in0=st[("ssv", i)][:], in1=neghalf[:, 0:3], op=ALU.pow)
-            nc.gpsimd.tensor_tensor(out=rr[:, 3:4], in0=st[("sss", i)][:], in1=neghalf[:, 3:4], op=ALU.pow)
-            nc.gpsimd.tensor_scalar(out=r[:], in0=rr[:], scalar1=1e12, scalar2=0.0, op0=ALU.min, op1=ALU.max)
-            st[("r", i)] = r
+            st[("r", i)] = small.tile([P, 4], F32, name="r", tag="r")
+            if i < 2:
+                nc.scalar.activation(out=st[("r", i)][:], in_=st[("cl", i)][:], func=ACT.Abs_reciprocal_sqrt)
+            else:
+                nc.gpsimd.tensor_tensor(out=st[("r", i)][:], in0=st[("cl", i)][:], in1=neghalf[:], op=ALU.pow)
 
         def TB(i):
-            if not ok(i):
-                return
             r = st[("r", i)]
             rb = psum.tile([P, 4, P], F32, name="rb", tag="bc", bufs=2)
             for col in range(4):
-                nc.tensor.transpose(out=rb[:, col, :], in_=r[:, col : col + 1].to_broadcast([P, P]), identity=ident_f[:])
+                nc.tensor.transpose(out=rb[:, col, :], in_=r[:, col : col + 1].to_broadcast([P, P]), identity=ident[:])
             st[("rb", i)] = rb
-            st[("gx", i)] = work.tile([P, CH, 4], BF16, name="gx", tag="gx", align_bytes=64, bufs=NB["gx"])
 
         def XR(i):
-            if not (ok(i) and within(GR_, i)):
-                return
-            rbs = work.tile([P, CH], F32, name="rbs", tag="rbs", bufs=NB["rbs"])
-            copy_out(not within(XRS, i), rbs[:], st[("rb", i)][:].rearrange("p k n -> p (k n)"))
+            rbs = work.tile([P, 256], F32, name="rbs", tag="rbs", bufs=2)
+            if i < NG:
+                nc.scalar.copy(out=rbs[:], in_=st[("rb", i)][:, 2:4, :].rearrange("p k n -> p (k n)"))
+            else:
+                nc.scalar.copy(
+                    out=rbs[:].rearrange("p (w e) -> p w e", e=2), in_=st[("rb", i)][:, 2:4, :].rearrange("p e w -> p w e")
+                )
             st[("rbs", i)] = rbs
 
-        def A5(i, k):
-            if not ok(i):
-                return
-            x_sb, c0 = xchunk(i)
+        def gx_of(i):
+            if ("gx", i) not in st:
+                st[("gx", i)] = work.tile([P, CH, 4], BF16, name="gx", tag="gx", align_bytes=64, bufs=2)
+            return st[("gx", i)]
+
+        def AV(i, k):
+            x_sb, words, wide, c0 = xloc[i]
             lo = P * k
-            if k in GP and within(GR_, i):
-                eng, rsrc = nc.gpsimd, st[("rbs", i)][:, lo : lo + P]
+            gx = gx_of(i)
+            rb = st[("rb", i)]
+            if i < NG:
+                nc.vector.tensor_tensor(
+                    out=gx[:, lo : lo + P, :],
+                    in0=rb[:, k, :].unsqueeze(2).to_broadcast([P, P, 4]),
+                    in1=x_sb[:, :, c0 + lo : c0 + lo + P].rearrange("p j n -> p n j"),
+                    op=ALU.mult,
+                )
             else:
-                eng, rsrc = nc.vector, st[("rb", i)][:, k, :]
-            eng.tensor_tensor(
-                out=st[("gx", i)][:, lo : lo + P, :],
-                in0=rsrc.unsqueeze(2).to_broadcast([P, P, 4]),
+                h, w0 = k // 2, 64 * (k % 2)
+                nc.vector.tensor_tensor(
+                    out=gx[:, lo : lo + P, :].rearrange("p (w e) j -> p w e j", e=2),
+                    in0=rb[:, 2 * h : 2 * h + 2, w0 : w0 + 64].rearrange("p e w -> p w e").unsqueeze(3).to_broadcast([P, 64, 2, 4]),
+                    in1=x_sb[:, :, c0 + lo : c0 + lo + P].rearrange("p j (w e) -> p w e j", e=2),
+                    op=ALU.mult,
+                )
+
+        def AG(i, k):
+            x_sb, words, wide, c0 = xloc[i]
+            lo = P * k
+            nc.gpsimd.tensor_tensor(
+                out=gx_of(i)[:, lo : lo + P, :],
+                in0=st[("rbs", i)][:, lo - 256 : lo - 128].unsqueeze(2).to_broadcast([P, P, 4]),
                 in1=x_sb[:, :, c0 + lo : c0 + lo + P].rearrange("p j n -> p n j"),
                 op=ALU.mult,
             )
 
-        def QF(i):
-            if not ok(i):
-                return
-            fnc = work.tile([P, CH], U32, name="fnc", tag="fnc", align_bytes=64, bufs=NB["fn"])
-            fns = work.tile([P, CH], U8, name="fns", tag="fns", align_bytes=64, bufs=NB["fn"])
-            nc.vector.quantize_mx(out=fnc[:].bitcast(FP8X4), scales=fns[:], in_=st[("gx", i)][:].rearrange("p n j -> p (n j)"))
-            st[("fn", i)] = (fnc, fns)
-        def M1(i, k):
-            if not ok(i):
-                return
+        def QF(i, lo, hi):
+            if ("fn", i) not in st:
+                fnc = work.tile([P, CH], U32, name="fnc", tag="fnc", align_bytes=64, bufs=2)
+                fns = work.tile([P, CH], U8, name="fns", tag="fns", align_bytes=64, bufs=2)
+                st[("fn", i)] = (fnc, fns)
             fnc, fns = st[("fn", i)]
-            if ("e", i) not in st:
-                st[("negm", i)] = small.tile([P, 4], F32, name="negm", tag="negm", bufs=NB["e"])
-                st[("z", i)] = small.tile([P, 4], F32, name="z", tag="z", bufs=NB["e"])
-                st[("e", i)] = work.tile([P, 4, K], BF16, name="e", tag="e", bufs=NB["e"])
+            nc.vector.quantize_mx(
+                out=fnc[:, lo:hi].bitcast(FP8X4), scales=fns[:, lo:hi], in_=st[("gx", i)][:, lo:hi, :].rearrange("p n j -> p (n j)")
+            )
+
+        def M1(i, k):
+            fnc, fns = st[("fn", i)]
+            if k == 0:
+                st[("negm", i)] = small.tile([P, 4], F32, name="negm", tag="negm")
+                st[("z", i)] = small.tile([P, 4], F32, name="z", tag="z")
+                st[("e", i)] = work.tile([P, 4, K], BF16, name="e", tag="e", bufs=2)
             sim = psum.tile([P, K], F32, name="sim", tag="sim", bufs=2)
             nc.tensor.matmul_mx(
                 out=sim[:],
@@ -218,15 +280,11 @@ def tile_memorybank2d_pa_t_kernel(tc, x, memory, out_0, out_1):
             st[("sim", i, k)] = sim
 
         def MAX(i, k):
-            if not ok(i):
-                return
             nc.vector.tensor_reduce(
                 out=st[("negm", i)][:, k : k + 1], in_=st[("sim", i, k)][:], axis=AX.X, op=ALU.max, negate=True
             )
 
         def EXP(i, k):
-            if not ok(i):
-                return
             nc.scalar.activation(
                 out=st[("e", i)][:, k, :],
                 in_=st[("sim", i, k)][:],
@@ -237,72 +295,60 @@ def tile_memorybank2d_pa_t_kernel(tc, x, memory, out_0, out_1):
             )
 
         def TE(i, h):
-            if not ok(i):
-                return
-            e = st[("e", i)]
+            ew = st[("e", i)][:].rearrange("p k s -> p (k s)").bitcast(F32)
             if h == 0:
-                st[("ge", i)] = work.tile([P, CH, 4], BF16, name="ge", tag="ge", align_bytes=64, bufs=NB["ge"])
-            et = psum.tile([P, 4, 256], BF16, name="et", tag="et", bufs=1)
+                st[("ge", i)] = work.tile([P, CH * 4], BF16, name="ge", tag="ge", align_bytes=64, bufs=2)
+            et = psum.tile([P, 2, 256], F32, name="et", tag="et", bufs=1)
             for bb in range(2):
-                for t in range(4):
-                    nc.tensor.transpose(
-                        out=et[:, t, P * bb : P * bb + P], in_=e[:, 2 * h + bb, P * t : P * t + P], identity=ident_b[:]
-                    )
+                for u in range(2):
+                    w0 = 256 * (2 * h + bb) + P * u
+                    nc.tensor.transpose(out=et[:, u, P * bb : P * bb + P], in_=ew[:, w0 : w0 + P], identity=ident[:])
             st[("et", i, h)] = et
 
         def XE(i, h):
-            if not ok(i):
-                return
-            et = st[("et", i, h)]
-            dst = st[("ge", i)][:, 256 * h : 256 * h + 256, :]
-            if ETG:
-                ets = work.tile([P, 4, 256], BF16, name="ets", tag="ets")
-                nc.scalar.copy(out=ets[:], in_=et[:])
-                nc.gpsimd.tensor_scalar(
-                    out=dst, in0=ets[:].rearrange("p t n -> p n t"), scalar1=1.0, scalar2=0.0, op0=ALU.mult, op1=ALU.add
-                )
-            else:
-                copy_out(within(XE1V if h else XE0V, i), dst, et[:].rearrange("p t n -> p n t"))
+            dst = st[("ge", i)][:].bitcast(F32)[:, 512 * h : 512 * h + 512]
+            nc.scalar.copy(out=dst.rearrange("p (n u) -> p n u", u=2), in_=st[("et", i, h)][:].rearrange("p u n -> p n u"))
+
+        def by_dma(i):
+            return NZ <= i < NCH - 2
 
         def RZ(i):
-            if not ok(i):
-                return
-            rz = small.tile([P, 4], F32, name="rz", tag="rz", bufs=NB["rz"])
-            nc.vector.reciprocal(out=rz[:], in_=st[("z", i)][:])
-            st[("rz", i)] = rz
+            nc.vector.reciprocal(out=rzw[i % 2][:, 0:4], in_=st[("z", i)][:])
 
         def TZ(i):
-            if not ok(i):
-                return
-            rz = st[("rz", i)]
+            rz = rzw[i % 2]
             rzp = psum.tile([P, 4, P], F32, name="rzp", tag="bc", bufs=2)
-            for k in range(4):
-                nc.tensor.transpose(out=rzp[:, k, :], in_=rz[:, k : k + 1].to_broadcast([P, P]), identity=ident_f[:])
+            if by_dma(i):
+                nc.tensor.transpose(out=rzp[:, 0, :], in_=rz[:], identity=ident[:])
+            else:
+                for k in range(4):
+                    nc.tensor.transpose(out=rzp[:, k, :], in_=rz[:, k : k + 1].to_broadcast([P, P]), identity=ident[:])
             st[("rzp", i)] = rzp
 
         def XZ(i):
-            if not ok(i):
-                return
             b, n0 = where(i)
-            rzb = work.tile([P, CH], F32, name="rzb", tag="rzb", bufs=NB["rzb"])
-            copy_out(within(XZV, i), rzb[:], st[("rzp", i)][:].rearrange("p k n -> p (k n)"))
-            nc.sync.dma_start(out=out_1.rearrange("b h w -> b (h w)")[b : b + 1, n0 : n0 + CH], in_=rzb[0:1, :])
+            rzb = work.tile([P, CH], F32, name="rzb", tag="rzb", bufs=3)
+            row = out_1.rearrange("b h w -> b (h w)")[b : b + 1, n0 : n0 + CH]
+            if by_dma(i):
+                zrow = small.tile([4, P], F32, name="zrow", tag="zrow")
+                nc.scalar.copy(out=zrow[:], in_=st[("rzp", i)][0:4, 0, :])
+                nc.sync.dma_start(out=row.rearrange("o (k n) -> (o k) n", k=4), in_=zrow[:])
+                nc.sync.dma_start(out=rzb[:], in_=row.rearrange("o n -> (o n)").partition_broadcast(P))
+            else:
+                nc.scalar.copy(out=rzb[:], in_=st[("rzp", i)][:].rearrange("p k n -> p (k n)"))
+                nc.sync.dma_start(out=row, in_=rzb[0:1, :])
             st[("rzb", i)] = rzb
 
         def QE(i):
-            if not ok(i):
-                return
-            ec = work.tile([P, CH], U32, name="ec", tag="ec", align_bytes=64, bufs=NB["ec"])
-            es = work.tile([P, CH], U8, name="es", tag="es", align_bytes=64, bufs=NB["ec"])
-            nc.vector.quantize_mx(out=ec[:].bitcast(FP8X4), scales=es[:], in_=st[("ge", i)][:].rearrange("p n t -> p (n t)"))
+            ec = work.tile([P, CH], U32, name="ec", tag="ec", align_bytes=64, bufs=2)
+            es = work.tile([P, CH], U8, name="es", tag="es", align_bytes=64, bufs=2)
+            nc.vector.quantize_mx(out=ec[:].bitcast(FP8X4), scales=es[:], in_=st[("ge", i)][:])
             st[("ec", i)] = (ec, es)
 
         def M2(i, cc):
-            if not ok(i):
-                return
             ec, es = st[("ec", i)]
-            if ("osb", i) not in st:
-                st[("osb", i)] = opool.tile([P, 4, CH], F32, name="osb", tag="osb", bufs=NB["osb"] + 1)
+            if cc == 0:
+                st[("osb", i)] = opool.tile([P, 4, CH], F32, name="osb", tag="osb")
             rec = psum.tile([P, CH], F32, name="rec", tag="rec", bufs=2)
             nc.tensor.matmul_mx(
                 out=rec[:],
@@ -316,8 +362,6 @@ def tile_memorybank2d_pa_t_kernel(tc, x, memory, out_0, out_1):
             st[("rec", i, cc)] = rec
 
         def D(i, cc):
-            if not ok(i):
-                return
             nc.vector.tensor_tensor(
                 out=st[("osb", i)][:, cc, :], in0=st[("rec", i, cc)][:], in1=st[("rzb", i)][:], op=ALU.mult
             )
@@ -326,109 +370,113 @@ def tile_memorybank2d_pa_t_kernel(tc, x, memory, out_0, out_1):
                 out=out_0[b].rearrange("(cc p) h w -> p cc (h w)", p=P)[:, cc, n0 : n0 + CH], in_=st[("osb", i)][:, cc, :]
             )
 
-        def MSQ():
-            for t in range(4):
-                nc.scalar.activation(out=junk[:], in_=mem[:, t, :], func=ACT.Square, accum_out=ssm[:, t : t + 1])
+        MSQS(0)
+        MSQV(2)
+        MSQS(1)
+        MSQV(3)
+        CM()
+        RM()
+        GR(0)
+        for k in range(4):
+            DG(0, k)
+        CL(0)
+        R(0)
+        for t in range(4):
+            MN(t)
+        GR(1)
+        TM(0)
+        TM(1)
+        for k in range(4):
+            DG(1, k)
+        CL(1)
+        R(1)
+        TB(0)
+        XM(0, nc.scalar.copy)
+        XM(1, nc.scalar.copy)
+        nc.scalar.activation(out=dummy[:], in_=one[:], func=ACT.Exp)
+        GR(2)
+        AV(0, 0)
+        AV(0, 1)
+        QM()
+        QF(0, 0, 256)
+        for k in range(4):
+            DG(2, k)
+        CL(2)
+        R(2)
+        G2(0)
+        G2(1)
 
-        def RM():
-            rsqrt_clamped(rm[:], ssmc[:], ssm[:])
+        plan = {}
 
-        def NJ():
-            for t in range(4):
-                nc.scalar.activation(
-                    out=mnj[:, t, :, :],
-                    in_=mem[:, t, :].rearrange("p (q j) -> p j q", j=4),
-                    func=ACT.Copy,
-                    scale=rm[:, t : t + 1],
-                )
+        def at(beat, op, *args):
+            plan.setdefault(beat, []).append((RANK.index(op), op, args))
 
-        def TM(h):
-            tm = psum.tile([P, 4, 256], BF16, name="tm", tag="sim", bufs=2)
-            for j in range(4):
-                for tt in range(2):
-                    nc.tensor.transpose(
-                        out=tm[:, j, P * tt : P * tt + P], in_=mnj[:, 2 * h + tt, j, :], identity=ident_b[:]
-                    )
-            st[("tm", h)] = tm
-
-        def XM(h):
-            nc.scalar.copy(out=gm[:, 256 * h : 256 * h + 256, :], in_=st[("tm", h)][:].rearrange("p j s -> p s j"))
-
-        def QM():
-            nc.vector.quantize_mx(out=mnTc[:].bitcast(FP8X4), scales=mnTs[:], in_=gm[:].rearrange("p s j -> p (s j)"))
-
-        def N2a():
-            for t in range(4):
-                nc.scalar.activation(out=mn[:, t, :], in_=mem[:, t, :], func=ACT.Copy, scale=rm[:, t : t + 1])
-
-        def N2b():
-            nc.scalar.copy(out=g2[:], in_=mn[:].rearrange("p t c -> p c t"))
-
-        def N2c():
-            nc.vector.quantize_mx(out=mn2c[:].bitcast(FP8X4), scales=mn2s[:], in_=g2[:].rearrange("p c t -> p (c t)"))
-
-        for s in range(NCH + 8):
-            M1(s - 5, 0)
-            if s == 5:
-                N2b()
-            if s == 1:
-                RM()
-            MAX(s - 5, 0)
-            EXP(s - 5, 0)
-            M2(s - 8, 0)
-            M1(s - 5, 1)
-            D(s - 8, 0)
-            M2(s - 8, 2)
-            GR(s)
-            A5(s - 3, 1)
-            if s == 1:
-                NJ()
-            if s == 4:
-                QM()
-            MAX(s - 5, 1)
-            QF(s - 4)
-            TB(s - 2)
-            D(s - 8, 2)
-            TE(s - 6, 0)
-            M1(s - 5, 3)
-            M2(s - 8, 1)
-            RZ(s - 6)
-            EXP(s - 5, 1)
-            R(s - 1)
-            if s == 0:
-                MSQ()
-            DG(s, 0)
-            M1(s - 5, 2)
-            TZ(s - 6)
-            if s == 2:
-                TM(1)
-            DG(s, 2)
-            XE(s - 6, 0)
-            if s == 3:
-                XM(1)
-            DG(s, 1)
-            TX(s)
-            XR(s - 2)
-            MAX(s - 5, 3)
-            QE(s - 7)
-            EXP(s - 5, 3)
-            M2(s - 8, 3)
-            MAX(s - 5, 2)
-            XZ(s - 6)
-            TE(s - 6, 1)
-            if s == 2:
-                N2a()
-            if s == 6:
-                N2c()
-            EXP(s - 5, 2)
-            if s == 3:
-                XM(0)
-            A5(s - 3, 3)
-            SQ(s)
-            XE(s - 6, 1)
-            D(s - 8, 1)
-            A5(s - 2, 0)
-            A5(s - 2, 2)
-            if s == 2:
-                TM(0)
-            D(s - 8, 3)
+        RANK = [M1, M2, MAX, EXP, D, GR, TE, TX, TB, TZ, DG, SQ, XR, XE, XZ, RZ, AV, QE, QF, CL, R, AG, Q2]
+        for i in range(NCH):
+            b = 4 * i
+            lm2 = min(LM2, ZM2 + i)
+            for k in range(4):
+                at(b + k, M1, i, k)
+                at(b + k, MAX, i, k)
+                at(b + k, EXP, i, k)
+                at(b + lm2 + DO[k], M2, i, k)
+                at(b + lm2 + DO[k], D, i, k)
+            for h in range(2):
+                at(b + LTE + 2 * h, TE, i, h)
+                at(b + LXE + 2 * h, XE, i, h)
+            at(b + LRZ, RZ, i)
+            at(b + LTZ, TZ, i)
+            at(b + LTZ, XZ, i)
+            at(b + LQE, QE, i)
+        at(0, AV, 0, 2)
+        at(0, AV, 0, 3)
+        at(0, QF, 0, 256, 512)
+        at(1, TB, 1)
+        at(1, AV, 1, 0)
+        at(1, AV, 1, 1)
+        at(2, AV, 1, 2)
+        at(2, AV, 1, 3)
+        at(2, QF, 1, 0, 512)
+        at(2, TB, 2)
+        at(2, XR, 2)
+        at(2, AG, 2, 2)
+        at(2, AG, 2, 3)
+        at(4, AV, 2, 0)
+        at(5, AV, 2, 1)
+        at(6, QF, 2, 0, 512)
+        at(1, GR, 3)
+        for k in range(4):
+            at(3, DG, 3, k)
+        at(3, CL, 3)
+        at(3, R, 3)
+        at(5, TB, 3)
+        at(6, XR, 3)
+        at(7, AV, 3, 0)
+        at(8, AV, 3, 1)
+        at(7, AG, 3, 2)
+        at(7, AG, 3, 3)
+        at(10, QF, 3, 0, 512)
+        for i in range(4, NCH):
+            b = 4 * i
+            if i < NG:
+                at(b + LSQ, GR, i)
+                for k in range(4):
+                    at(b + LSQ + k, DG, i, k)
+            else:
+                for h in range(2):
+                    at(b + LSQ + TO[h], TX, i, h)
+                    at(b + LSQ + SO[2 * h], SQ, i, h, 0)
+                    at(b + LSQ + SO[2 * h + 1], SQ, i, h, 1)
+            at(b + LCL, CL, i)
+            at(b + LCL, R, i)
+            at(b + LTB, TB, i)
+            at(b + LXR, XR, i)
+            at(b + LAV, AV, i, 0)
+            at(b + LAV + 1, AV, i, 1)
+            at(b + LAG, AG, i, 2)
+            at(b + LAG, AG, i, 3)
+            at(b + LQF, QF, i, 0, 512)
+        at(LQE, Q2)
+        for beat in sorted(plan):
+            for rank, op, args in sorted(plan[beat], key=lambda p: p[0]):
+                op(*args)

from contextlib import ExitStack

import concourse.mybir as mybir
from concourse.masks import make_identity

F32 = mybir.dt.float32
BF16 = mybir.dt.bfloat16
U32 = mybir.dt.uint32
U8 = mybir.dt.uint8
FP8X4 = mybir.dt.float8_e4m3fn_x4
ALU = mybir.AluOpType
ACT = mybir.ActivationFunctionType
AX = mybir.AxisListType

P = 128
B, C, HW, K = 2, 512, 4096, 512
CH = 512
NCH = B * HW // CH
LOADS = (512, 512) + (1024,) * 7
FLOPS = 2 * 2 * B * HW * C * K
LM2 = 10
ZM2 = 7
NZ = 3
LSQ = -14
LCL = -10
LTB = -6
LXR = -6
LTZ = 5
LRZ = 4
LAV = -5
LQE = 6
LQF = -2
LAG = -5
NG = 4
LTE = 2
LXE = 2
DO = (0, 1, 2, 3)
TO = (0, 2)
SO = (0, 1, 2, 3)


def tile_memorybank2d_pa_t_kernel(tc, x, memory, out_0, out_1):
    nc = tc.nc
    with ExitStack() as ctx:
        const = ctx.enter_context(tc.tile_pool(name="const", bufs=1))
        xpool = ctx.enter_context(tc.tile_pool(name="xpool", bufs=1))
        small = ctx.enter_context(tc.tile_pool(name="small", bufs=3))
        work = ctx.enter_context(tc.tile_pool(name="work", bufs=3))
        opool = ctx.enter_context(tc.tile_pool(name="opool", bufs=3))
        psum = ctx.enter_context(tc.psum_pool(name="psum", bufs=1))
        ctx.enter_context(tc.manual_schedule())

        mem = const.tile([P, 4, C], BF16, name="mem")
        nc.sync.dma_start(out=mem[:], in_=memory.rearrange("(p t) c -> p t c", t=4))
        xloc = []
        for ld, width in enumerate(LOADS):
            first = len(xloc) * CH
            b, n0 = first // HW, first % HW
            x_sb = xpool.tile([P, 4, width], BF16, name="x%d" % ld)
            src = x[b].rearrange("(p j) h w -> p j (h w)", j=4)
            step = 256 if ld == 0 else width
            for c0 in range(0, width, step):
                nc.sync.dma_start(out=x_sb[:, :, c0 : c0 + step], in_=src[:, :, n0 + c0 : n0 + c0 + step])
            words = x_sb[:].rearrange("p j n -> p (j n)").bitcast(F32)
            xloc.extend([(x_sb, words, width // 2, c0) for c0 in range(0, width, CH)])

        neghalf = const.tile([P, 4], F32, name="neghalf")
        nc.vector.memset(neghalf[:], -0.5)
        ident = const.tile([P, P], F32, name="ident")
        make_identity(nc, ident[:])
        junk = const.tile([P, 512], BF16, name="junk")
        junkf = const.tile([P, 512], F32, name="junkf")
        dummy = const.tile([P, 1], F32, name="dummy")
        one = const.tile([P, 1], F32, name="one")
        nc.vector.memset(one[:], 1.0)
        nc.scalar.activation(out=dummy[:], in_=one[:], func=ACT.Abs_reciprocal_sqrt)

        mn = const.tile([P, 4, C], BF16, name="mn")
        g2 = const.tile([P, C, 4], BF16, name="g2", align_bytes=64)
        gm = const.tile([P, K * 4], BF16, name="gm", align_bytes=64)
        mn2c = const.tile([P, C], U32, name="mn2c", align_bytes=64)
        mn2s = const.tile([P, C], U8, name="mn2s", align_bytes=64)
        mnTc = const.tile([P, K], U32, name="mnTc", align_bytes=64)
        mnTs = const.tile([P, K], U8, name="mnTs", align_bytes=64)
        ssm = const.tile([P, 4], F32, name="ssm")
        rzw = [const.tile([P, P], F32, name="rzw%d" % n) for n in range(2)]
        for n in range(2):
            nc.gpsimd.memset(rzw[n][:], 0.0)
        mn_words = mn[:].rearrange("p t c -> p (t c)").bitcast(F32)

        st = {}

        def clamp(ss):
            clamped = small.tile([P, 4], F32, name="clamped", tag="clamped")
            nc.vector.tensor_scalar(out=clamped[:], in0=ss, scalar1=1e-24, scalar2=None, op0=ALU.max)
            return clamped

        def MSQS(t):
            nc.scalar.activation(out=junk[:], in_=mem[:, t, :], func=ACT.Square, accum_out=ssm[:, t : t + 1])

        def MSQV(t):
            nc.vector.scalar_tensor_tensor(
                out=junkf[:], in0=mem[:, t, :], scalar=1.0, in1=mem[:, t, :], op0=ALU.mult, op1=ALU.mult, accum_out=ssm[:, t : t + 1]
            )

        def CM():
            st["cm"] = clamp(ssm[:])

        def RM():
            st["rm"] = const.tile([P, 4], F32, name="rm")
            nc.scalar.activation(out=st["rm"][:], in_=st["cm"][:], func=ACT.Abs_reciprocal_sqrt)

        def MN(t):
            nc.vector.tensor_scalar(
                out=mn[:, t, :], in0=mem[:, t, :], scalar1=st["rm"][:, t : t + 1], scalar2=None, op0=ALU.mult
            )

        def TM(u):
            tm = psum.tile([P, 2, 2, P], F32, name="tm", tag="sim", bufs=2)
            for e in range(2):
                for v in range(2):
                    first = (2 * u + e) * (C // 2) + v
                    nc.tensor.transpose(out=tm[:, e, v, :], in_=mn_words[:, first : first + 255 : 2], identity=ident[:])
            st[("tm", u)] = tm

        def XM(u, eng):
            dst = gm[:].bitcast(F32)[:, 512 * u : 512 * u + 512]
            eng(out=dst.rearrange("p (q e v) -> p q e v", e=2, v=2), in_=st[("tm", u)][:].rearrange("p e v q -> p q e v"))

        def QM():
            nc.vector.quantize_mx(out=mnTc[:].bitcast(FP8X4), scales=mnTs[:], in_=gm[:])

        def G2(h):
            nc.gpsimd.tensor_scalar(
                out=g2[:, 256 * h : 256 * h + 256, :],
                in0=mn[:, :, 256 * h : 256 * h + 256].rearrange("p t c -> p c t"),
                scalar1=1.0,
                scalar2=0.0,
                op0=ALU.mult,
                op1=ALU.add,
            )

        def Q2():
            nc.vector.quantize_mx(out=mn2c[:].bitcast(FP8X4), scales=mn2s[:], in_=g2[:].rearrange("p c t -> p (c t)"))

        def ok(i):
            return 0 <= i < NCH

        def where(i):
            return i // (HW // CH), (i % (HW // CH)) * CH

        def GR(i):
            x_sb, words, wide, c0 = xloc[i]
            gr = psum.tile([P, 4, P], F32, name="gr", tag="rec", bufs=2)
            st[("ss", i)] = small.tile([P, 4], F32, name="ss", tag="ss")
            for k in range(4):
                for j in range(4):
                    blk = x_sb[:, j, c0 + P * k : c0 + P * k + P]
                    nc.tensor.matmul(out=gr[:, k, :], lhsT=blk, rhs=blk, start=(j == 0), stop=(j == 3))
            st[("gr", i)] = gr

        def DG(i, k):
            nc.vector.scalar_tensor_tensor(
                out=junkf[:, 0:P],
                in0=st[("gr", i)][:, k, :],
                scalar=1.0,
                in1=ident[:],
                op0=ALU.mult,
                op1=ALU.mult,
                accum_out=st[("ss", i)][:, k : k + 1],
            )

        def TX(i, h):
            x_sb, words, wide, c0 = xloc[i]
            if h == 0:
                st[("ss", i)] = small.tile([P, 4], F32, name="ss", tag="ss")
            xt = psum.tile([P, 512], F32, name="xt", tag="xt", bufs=1)
            for j in range(4):
                w0 = j * wide + c0 // 2 + P * h
                nc.tensor.transpose(out=xt[:, P * j : P * j + P], in_=words[:, w0 : w0 + P], identity=ident[:])
            st[("xt", i, h)] = xt

        def SQ(i, h, e):
            nc.scalar.activation(
                out=junk[:],
                in_=st[("xt", i, h)][:].bitcast(BF16).rearrange("p (m e) -> p e m", e=2)[:, e, :],
                func=ACT.Square,
                accum_out=st[("ss", i)][:, 2 * h + e : 2 * h + e + 1],
            )

        def CL(i):
            st[("cl", i)] = clamp(st[("ss", i)][:])

        def R(i):
            st[("r", i)] = small.tile([P, 4], F32, name="r", tag="r")
            if i < 2:
                nc.scalar.activation(out=st[("r", i)][:], in_=st[("cl", i)][:], func=ACT.Abs_reciprocal_sqrt)
            else:
                nc.gpsimd.tensor_tensor(out=st[("r", i)][:], in0=st[("cl", i)][:], in1=neghalf[:], op=ALU.pow)

        def TB(i):
            r = st[("r", i)]
            rb = psum.tile([P, 4, P], F32, name="rb", tag="bc", bufs=2)
            for col in range(4):
                nc.tensor.transpose(out=rb[:, col, :], in_=r[:, col : col + 1].to_broadcast([P, P]), identity=ident[:])
            st[("rb", i)] = rb

        def XR(i):
            rbs = work.tile([P, 256], F32, name="rbs", tag="rbs", bufs=2)
            if i < NG:
                nc.scalar.copy(out=rbs[:], in_=st[("rb", i)][:, 2:4, :].rearrange("p k n -> p (k n)"))
            else:
                nc.scalar.copy(
                    out=rbs[:].rearrange("p (w e) -> p w e", e=2), in_=st[("rb", i)][:, 2:4, :].rearrange("p e w -> p w e")
                )
            st[("rbs", i)] = rbs

        def gx_of(i):
            if ("gx", i) not in st:
                st[("gx", i)] = work.tile([P, CH, 4], BF16, name="gx", tag="gx", align_bytes=64, bufs=2)
            return st[("gx", i)]

        def AV(i, k):
            x_sb, words, wide, c0 = xloc[i]
            lo = P * k
            gx = gx_of(i)
            rb = st[("rb", i)]
            if i < NG:
                nc.vector.tensor_tensor(
                    out=gx[:, lo : lo + P, :],
                    in0=rb[:, k, :].unsqueeze(2).to_broadcast([P, P, 4]),
                    in1=x_sb[:, :, c0 + lo : c0 + lo + P].rearrange("p j n -> p n j"),
                    op=ALU.mult,
                )
            else:
                h, w0 = k // 2, 64 * (k % 2)
                nc.vector.tensor_tensor(
                    out=gx[:, lo : lo + P, :].rearrange("p (w e) j -> p w e j", e=2),
                    in0=rb[:, 2 * h : 2 * h + 2, w0 : w0 + 64].rearrange("p e w -> p w e").unsqueeze(3).to_broadcast([P, 64, 2, 4]),
                    in1=x_sb[:, :, c0 + lo : c0 + lo + P].rearrange("p j (w e) -> p w e j", e=2),
                    op=ALU.mult,
                )

        def AG(i, k):
            x_sb, words, wide, c0 = xloc[i]
            lo = P * k
            nc.gpsimd.tensor_tensor(
                out=gx_of(i)[:, lo : lo + P, :],
                in0=st[("rbs", i)][:, lo - 256 : lo - 128].unsqueeze(2).to_broadcast([P, P, 4]),
                in1=x_sb[:, :, c0 + lo : c0 + lo + P].rearrange("p j n -> p n j"),
                op=ALU.mult,
            )

        def QF(i, lo, hi):
            if ("fn", i) not in st:
                fnc = work.tile([P, CH], U32, name="fnc", tag="fnc", align_bytes=64, bufs=2)
                fns = work.tile([P, CH], U8, name="fns", tag="fns", align_bytes=64, bufs=2)
                st[("fn", i)] = (fnc, fns)
            fnc, fns = st[("fn", i)]
            nc.vector.quantize_mx(
                out=fnc[:, lo:hi].bitcast(FP8X4), scales=fns[:, lo:hi], in_=st[("gx", i)][:, lo:hi, :].rearrange("p n j -> p (n j)")
            )

        def M1(i, k):
            fnc, fns = st[("fn", i)]
            if k == 0:
                st[("negm", i)] = small.tile([P, 4], F32, name="negm", tag="negm")
                st[("z", i)] = small.tile([P, 4], F32, name="z", tag="z")
                st[("e", i)] = work.tile([P, 4, K], BF16, name="e", tag="e", bufs=2)
            sim = psum.tile([P, K], F32, name="sim", tag="sim", bufs=2)
            nc.tensor.matmul_mx(
                out=sim[:],
                lhsT=fnc[:, P * k : P * k + P].bitcast(FP8X4),
                lhsT_scale=fns[:, P * k : P * k + P],
                rhs=mnTc[:].bitcast(FP8X4),
                rhs_scale=mnTs[:],
                start=True,
                stop=True,
            )
            st[("sim", i, k)] = sim

        def MAX(i, k):
            nc.vector.tensor_reduce(
                out=st[("negm", i)][:, k : k + 1], in_=st[("sim", i, k)][:], axis=AX.X, op=ALU.max, negate=True
            )

        def EXP(i, k):
            nc.scalar.activation(
                out=st[("e", i)][:, k, :],
                in_=st[("sim", i, k)][:],
                func=ACT.Exp,
                bias=st[("negm", i)][:, k : k + 1],
                scale=1.0,
                accum_out=st[("z", i)][:, k : k + 1],
            )

        def TE(i, h):
            ew = st[("e", i)][:].rearrange("p k s -> p (k s)").bitcast(F32)
            if h == 0:
                st[("ge", i)] = work.tile([P, CH * 4], BF16, name="ge", tag="ge", align_bytes=64, bufs=2)
            et = psum.tile([P, 2, 256], F32, name="et", tag="et", bufs=1)
            for bb in range(2):
                for u in range(2):
                    w0 = 256 * (2 * h + bb) + P * u
                    nc.tensor.transpose(out=et[:, u, P * bb : P * bb + P], in_=ew[:, w0 : w0 + P], identity=ident[:])
            st[("et", i, h)] = et

        def XE(i, h):
            dst = st[("ge", i)][:].bitcast(F32)[:, 512 * h : 512 * h + 512]
            nc.scalar.copy(out=dst.rearrange("p (n u) -> p n u", u=2), in_=st[("et", i, h)][:].rearrange("p u n -> p n u"))

        def by_dma(i):
            return NZ <= i < NCH - 2

        def RZ(i):
            nc.vector.reciprocal(out=rzw[i % 2][:, 0:4], in_=st[("z", i)][:])

        def TZ(i):
            rz = rzw[i % 2]
            rzp = psum.tile([P, 4, P], F32, name="rzp", tag="bc", bufs=2)
            if by_dma(i):
                nc.tensor.transpose(out=rzp[:, 0, :], in_=rz[:], identity=ident[:])
            else:
                for k in range(4):
                    nc.tensor.transpose(out=rzp[:, k, :], in_=rz[:, k : k + 1].to_broadcast([P, P]), identity=ident[:])
            st[("rzp", i)] = rzp

        def XZ(i):
            b, n0 = where(i)
            rzb = work.tile([P, CH], F32, name="rzb", tag="rzb", bufs=3)
            row = out_1.rearrange("b h w -> b (h w)")[b : b + 1, n0 : n0 + CH]
            if by_dma(i):
                zrow = small.tile([4, P], F32, name="zrow", tag="zrow")
                nc.scalar.copy(out=zrow[:], in_=st[("rzp", i)][0:4, 0, :])
                nc.sync.dma_start(out=row.rearrange("o (k n) -> (o k) n", k=4), in_=zrow[:])
                nc.sync.dma_start(out=rzb[:], in_=row.rearrange("o n -> (o n)").partition_broadcast(P))
            else:
                nc.scalar.copy(out=rzb[:], in_=st[("rzp", i)][:].rearrange("p k n -> p (k n)"))
                nc.sync.dma_start(out=row, in_=rzb[0:1, :])
            st[("rzb", i)] = rzb

        def QE(i):
            ec = work.tile([P, CH], U32, name="ec", tag="ec", align_bytes=64, bufs=2)
            es = work.tile([P, CH], U8, name="es", tag="es", align_bytes=64, bufs=2)
            nc.vector.quantize_mx(out=ec[:].bitcast(FP8X4), scales=es[:], in_=st[("ge", i)][:])
            st[("ec", i)] = (ec, es)

        def M2(i, cc):
            ec, es = st[("ec", i)]
            if cc == 0:
                st[("osb", i)] = opool.tile([P, 4, CH], F32, name="osb", tag="osb")
            rec = psum.tile([P, CH], F32, name="rec", tag="rec", bufs=2)
            nc.tensor.matmul_mx(
                out=rec[:],
                lhsT=mn2c[:, P * cc : P * cc + P].bitcast(FP8X4),
                lhsT_scale=mn2s[:, P * cc : P * cc + P],
                rhs=ec[:].bitcast(FP8X4),
                rhs_scale=es[:],
                start=True,
                stop=True,
            )
            st[("rec", i, cc)] = rec

        def D(i, cc):
            nc.vector.tensor_tensor(
                out=st[("osb", i)][:, cc, :], in0=st[("rec", i, cc)][:], in1=st[("rzb", i)][:], op=ALU.mult
            )
            b, n0 = where(i)
            nc.sync.dma_start(
                out=out_0[b].rearrange("(cc p) h w -> p cc (h w)", p=P)[:, cc, n0 : n0 + CH], in_=st[("osb", i)][:, cc, :]
            )

        MSQS(0)
        MSQV(2)
        MSQS(1)
        MSQV(3)
        CM()
        RM()
        GR(0)
        for k in range(4):
            DG(0, k)
        CL(0)
        R(0)
        for t in range(4):
            MN(t)
        GR(1)
        TM(0)
        TM(1)
        for k in range(4):
            DG(1, k)
        CL(1)
        R(1)
        TB(0)
        XM(0, nc.scalar.copy)
        XM(1, nc.scalar.copy)
        nc.scalar.activation(out=dummy[:], in_=one[:], func=ACT.Exp)
        GR(2)
        AV(0, 0)
        AV(0, 1)
        QM()
        QF(0, 0, 256)
        for k in range(4):
            DG(2, k)
        CL(2)
        R(2)
        G2(0)
        G2(1)

        plan = {}

        def at(beat, op, *args):
            plan.setdefault(beat, []).append((RANK.index(op), op, args))

        RANK = [M1, M2, MAX, EXP, D, GR, TE, TX, TB, TZ, DG, SQ, XR, XE, XZ, RZ, AV, QE, QF, CL, R, AG, Q2]
        for i in range(NCH):
            b = 4 * i
            lm2 = min(LM2, ZM2 + i)
            for k in range(4):
                at(b + k, M1, i, k)
                at(b + k, MAX, i, k)
                at(b + k, EXP, i, k)
                at(b + lm2 + DO[k], M2, i, k)
                at(b + lm2 + DO[k], D, i, k)
            for h in range(2):
                at(b + LTE + 2 * h, TE, i, h)
                at(b + LXE + 2 * h, XE, i, h)
            at(b + LRZ, RZ, i)
            at(b + LTZ, TZ, i)
            at(b + LTZ, XZ, i)
            at(b + LQE, QE, i)
        at(0, AV, 0, 2)
        at(0, AV, 0, 3)
        at(0, QF, 0, 256, 512)
        at(1, TB, 1)
        at(1, AV, 1, 0)
        at(1, AV, 1, 1)
        at(2, AV, 1, 2)
        at(2, AV, 1, 3)
        at(2, QF, 1, 0, 512)
        at(2, TB, 2)
        at(2, XR, 2)
        at(2, AG, 2, 2)
        at(2, AG, 2, 3)
        at(4, AV, 2, 0)
        at(5, AV, 2, 1)
        at(6, QF, 2, 0, 512)
        at(1, GR, 3)
        for k in range(4):
            at(3, DG, 3, k)
        at(3, CL, 3)
        at(3, R, 3)
        at(5, TB, 3)
        at(6, XR, 3)
        at(7, AV, 3, 0)
        at(8, AV, 3, 1)
        at(7, AG, 3, 2)
        at(7, AG, 3, 3)
        at(10, QF, 3, 0, 512)
        for i in range(4, NCH):
            b = 4 * i
            if i < NG:
                at(b + LSQ, GR, i)
                for k in range(4):
                    at(b + LSQ + k, DG, i, k)
            else:
                for h in range(2):
                    at(b + LSQ + TO[h], TX, i, h)
                    at(b + LSQ + SO[2 * h], SQ, i, h, 0)
                    at(b + LSQ + SO[2 * h + 1], SQ, i, h, 1)
            at(b + LCL, CL, i)
            at(b + LCL, R, i)
            at(b + LTB, TB, i)
            at(b + LXR, XR, i)
            at(b + LAV, AV, i, 0)
            at(b + LAV + 1, AV, i, 1)
            at(b + LAG, AG, i, 2)
            at(b + LAG, AG, i, 3)
            at(b + LQF, QF, i, 0, 512)
        at(LQE, Q2)
        for beat in sorted(plan):
            for rank, op, args in sorted(plan[beat], key=lambda p: p[0]):
                op(*args)
